import numpy as np
import ml_dtypes


def mxq(x, axis, fmt="e4m3"):
    dtype, down = {"e4m3": (ml_dtypes.float8_e4m3fn, 7), "e5m2": (ml_dtypes.float8_e5m2, 14)}[fmt]
    v = np.moveaxis(np.asarray(x, np.float32).astype(ml_dtypes.bfloat16).astype(np.float64), axis, -1)
    blocks = v.reshape(v.shape[:-1] + (-1, 32))
    amax = np.abs(blocks).max(-1, keepdims=True)
    byte = np.maximum(np.where(amax > 0, np.frexp(amax)[1] - 1 + 127, 0) - down, 1)
    scale = np.exp2(byte - 127.0)
    codes = (blocks / scale).astype(np.float32).astype(dtype).astype(np.float64)
    return np.moveaxis((codes * scale).reshape(v.shape), -1, axis)


WIDE = False


def mx_kscale(k):
    if not WIDE:
        return np.ones(k)
    levels = np.array([20, -20, 10, -10, 0])
    a = np.random.permutation(np.resize(levels, k // 512 * 4)).reshape(k // 512, 4)
    idx = np.arange(k)
    return np.exp2(a[idx // 512, idx % 128 // 32])


BF16 = ml_dtypes.bfloat16


def bf(x):
    return np.asarray(x, np.float32).astype(BF16)


def f64(x):
    return np.asarray(x).astype(np.float64)


B, C, H, W, OC = 2, 999, 32, 32, 1024
CS = 5
PAD = CS // 2
EPS = 1e-12
INC = C + CS * CS
CELL = 4
GSC = 8.0
KINK = 1e-3


def unit(f):
    n = np.maximum(np.sqrt(np.sum(f * f, axis=1, keepdims=True)), EPS)
    return f / n, n


def preact(feature, conv_w, conv_b):
    f, wt, bias = f64(feature), f64(conv_w), f64(conv_b)
    b, c, h, w = f.shape
    fn, _ = unit(f)
    fp = np.pad(fn, ((0, 0), (0, 0), (PAD, PAD), (PAD, PAD)))
    sims = []
    for cc in range(CS):
        for r in range(CS):
            sims.append(np.sum(fp[:, :, r:h + r, cc:w + cc] * fn, axis=1))
    x = np.concatenate([f, np.stack(sims, axis=1)], axis=1).reshape(b, c + CS * CS, h * w)
    return (wt @ x).reshape(b, wt.shape[0], h, w) + bias[None, :, None, None]


def setup_inputs():
    u = np.asarray(mx_kscale(OC), dtype=np.float64)
    coarse = np.random.standard_normal((B, C, H // CELL, W // CELL))
    feature = bf(0.7 * (np.random.standard_normal((B, C, H, W)) + np.repeat(np.repeat(coarse, CELL, axis=2), CELL, axis=3)))
    wsc = np.concatenate([np.full(C, 1.0 / np.sqrt(C)), np.full(CS * CS, 0.3)])
    conv_w0 = bf(np.random.standard_normal((OC, INC)) * wsc)
    conv_b = bf(np.random.standard_normal(OC) * 0.3)
    z = preact(feature, conv_w0, conv_b)
    g = np.random.standard_normal((B, OC, H, W)) * np.exp2(np.random.randint(-12, 1, (B, 1, H, W))) * GSC
    g = g * (np.abs(z) > KINK)
    return {"feature": feature, "conv_w": bf(f64(conv_w0) / u[:, None]), "conv_b": conv_b,
            "z": np.asarray(z, np.float32), "grad_out": bf(g * u[None, :, None, None])}


def reference(feature, conv_w, conv_b, z, grad_out):
    f = f64(feature)
    b, c, h, w = f.shape
    oc = conv_w.shape[0]
    dz = f64(grad_out) * (f64(z) > 0.0)
    dzq = mxq(dz.reshape(b, oc, h * w), 1, "e5m2")
    dx = (mxq(f64(conv_w), 0, "e4m3").T @ dzq).reshape(b, c + CS * CS, h, w)
    dv = dx[:, c:]
    fn, n = unit(f)
    fp = np.pad(fn, ((0, 0), (0, 0), (PAD, PAD), (PAD, PAD)))
    dfn = np.zeros_like(fn)
    dfp = np.zeros_like(fp)
    k = 0
    for cc in range(CS):
        for r in range(CS):
            d = dv[:, k:k + 1]
            dfn += d * fp[:, :, r:h + r, cc:w + cc]
            dfp[:, :, r:h + r, cc:w + cc] += d * fn
            k += 1
    dfn += dfp[:, :, PAD:PAD + h, PAD:PAD + w]
    dot = np.sum(dfn * fn, axis=1, keepdims=True)
    return dx[:, :c] + (dfn - fn * dot) / n

@@ -1,0 +1,456 @@
+from contextlib import ExitStack
+
+import concourse.mybir as mybir
+from concourse.masks import make_identity
+
+F32 = mybir.dt.float32
+BF16 = mybir.dt.bfloat16
+U32 = mybir.dt.uint32
+U8 = mybir.dt.uint8
+E4M3X4 = mybir.dt.float8_e4m3fn_x4
+E5M2X4 = mybir.dt.float8_e5m2_x4
+ALU = mybir.AluOpType
+ACT = mybir.ActivationFunctionType
+AX = mybir.AxisListType
+
+P = 128
+B, C, OC, HW = 2, 999, 1024, 1024
+CS = 5
+PAD = CS // 2
+NK = CS * CS
+CENTRE = NK // 2
+INC = C + NK
+EPS = 1e-12
+PACK = 4
+K_PASS = P * PACK
+PASSES = OC // K_PASS
+NT = INC // P
+C_TAIL = C - (NT - 1) * P
+ZERO_FROM = 96
+WORDS = HW // 2
+ROW_WORDS = 16
+GROUPS = WORDS // P
+NG = B * GROUPS
+HALF = 512
+F_PAD = 128
+R_PAD = 64
+RN_ROW = C_TAIL - 1
+
+FLOPS = 2 * OC * INC * B * HW + 4 * NK * C * B * HW
+
+
+def tile_spatialcontext_t_v_kernel(tc, feature, conv_w, conv_b, z, grad_out, out):
+    nc = tc.nc
+    feat = feature.rearrange("b c h w -> b c (h w)")
+    z_in = z.rearrange("b o h w -> b o (h w)")
+    g_in = grad_out.rearrange("b o h w -> b o (h w)")
+    res = out.rearrange("b c h w -> b c (h w)")
+
+    with ExitStack() as ctx:
+        keep = ctx.enter_context(tc.tile_pool(name="keep", bufs=1))
+        psum_v = ctx.enter_context(tc.psum_pool(name="psum_v", bufs=3))
+        psum_s = ctx.enter_context(tc.psum_pool(name="psum_s", bufs=2))
+        psum_mx = ctx.enter_context(tc.psum_pool(name="psum_mx", bufs=1))
+        psum_o = ctx.enter_context(tc.psum_pool(name="psum_o", bufs=1))
+        psum_c = ctx.enter_context(tc.psum_pool(name="psum_c", bufs=1))
+
+        ident = keep.tile([P, P], F32)
+        make_identity(nc, ident[:])
+
+        ident_rows = ident[:].rearrange("p (r u) -> p r u", u=ROW_WORDS)
+        at_edge = keep.tile([P, 2], F32)
+        nc.vector.tensor_reduce(out=at_edge[:, 0:1], in_=ident_rows[:, :, 0], axis=AX.X, op=ALU.add)
+        nc.vector.tensor_reduce(
+            out=at_edge[:, 1:2], in_=ident_rows[:, :, ROW_WORDS - 1], axis=AX.X, op=ALU.add
+        )
+        inside = keep.tile([P, 2], F32)
+        nc.vector.tensor_scalar(
+            out=inside[:], in0=at_edge[:], scalar1=-1.0, scalar2=1.0, op0=ALU.mult, op1=ALU.add
+        )
+        in_row = keep.tile([P, 2, NK], F32)
+        nc.vector.memset(in_row[:], 1.0)
+        for e in range(2):
+            for cc in range(CS):
+                wsh = (e + cc - PAD) // 2
+                if wsh != 0:
+                    side = 0 if wsh < 0 else 1
+                    nc.vector.tensor_copy(
+                        out=in_row[:, e, CS * cc : CS * (cc + 1)],
+                        in_=inside[:, side : side + 1].to_broadcast([P, CS]),
+                    )
+
+        f_sb = keep.tile([P, 2 * F_PAD + B * NT * HW], BF16)
+        f_words = f_sb[:].bitcast(F32)
+        nc.vector.memset(f_sb[:, 0:F_PAD], 0.0)
+        nc.vector.memset(f_sb[:, F_PAD + B * NT * HW :], 0.0)
+        for b in range(B):
+            last = F_PAD + (b * NT + NT - 1) * HW
+            nc.vector.memset(f_sb[ZERO_FROM:P, last : last + HW], 0.0)
+
+        w_codes = keep.tile([P, PASSES, INC], U32, align_bytes=64)
+        w_scales = keep.tile([P, PASSES, INC], U8, align_bytes=64)
+        dz_codes = keep.tile([P, B, PASSES, HW], U32, align_bytes=64)
+        dz_scales = keep.tile([P, B, PASSES, HW], U8, align_bytes=64)
+        own = keep.tile([P, 2 * NG, P], F32)
+        rows = keep.tile([P, B, 2, 2 * R_PAD + WORDS], F32)
+        nc.gpsimd.memset(rows[:], 0.0)
+        f_own = keep.tile([P, NG, 2 * INC], BF16)
+        alpha = keep.tile([P, 2 * NG, NK], F32)
+        sq_half = keep.tile([P, 2 * NG, 2], F32)
+        sq = keep.tile([P, 2 * NG], F32)
+        sq_floor = keep.tile([P, 2 * NG], F32)
+        norm = keep.tile([P, 2 * NG], F32)
+        rn = keep.tile([P, 2 * NG], F32)
+        rn2 = keep.tile([P, 2 * NG], F32)
+        neg_rn2 = keep.tile([P, 2 * NG], F32)
+        off_unit = keep.tile([P, 2 * NG], F32)
+        centre = keep.tile([P, 2 * NG], F32)
+
+        def word_window(pool, g, dy, wsh, half):
+            b, d = divmod(g, GROUPS)
+            bank = pool.tile([P, HALF], F32, tag="window", name="window")
+            for u in range(HALF // P):
+                t = half * (HALF // P) + u
+                w0 = F_PAD // 2 + (b * NT + t) * WORDS + P * d + wsh + ROW_WORDS * dy
+                nc.tensor.transpose(
+                    out=bank[:, u * P : (u + 1) * P], in_=f_words[:, w0 : w0 + P], identity=ident[:]
+                )
+            return bank
+
+        def pixel_of_words(words, ep, width):
+            return words.bitcast(BF16).rearrange("p (c e) -> p c e", e=2)[:, 0:width, ep]
+
+        def dx_group(g, e, half, bank):
+            b, d = divmod(g, GROUPS)
+            cols = slice(e * WORDS + d * P, e * WORDS + (d + 1) * P)
+            for c in range(PASSES):
+                nc.tensor.matmul_mx(
+                    out=bank[:],
+                    lhsT=dz_codes[:, b, c, cols].bitcast(E5M2X4),
+                    lhsT_scale=dz_scales[:, b, c, cols],
+                    rhs=w_codes[:, c, half * HALF : (half + 1) * HALF].bitcast(E4M3X4),
+                    rhs_scale=w_scales[:, c, half * HALF : (half + 1) * HALF],
+                    start=(c == 0),
+                    stop=(c == PASSES - 1),
+                )
+
+        with tc.tile_pool(name="stage_w", bufs=1) as stage_w, tc.tile_pool(
+            name="stage_z", bufs=2
+        ) as stage_z:
+            w_raw = stage_w.tile([P, PASSES, PACK, INC], BF16)
+            nc.sync.dma_start(
+                out=w_raw[:], in_=conv_w.rearrange("(c p j) i -> p c j i", p=P, j=PACK)
+            )
+            for b in range(B):
+                base = F_PAD + b * NT * HW
+                nc.sync.dma_start(
+                    out=f_sb[:, base : base + (NT - 1) * HW].rearrange("p (t x) -> p t x", x=HW),
+                    in_=feat[b, 0 : (NT - 1) * P, :].rearrange("(t p) x -> p t x", p=P),
+                )
+                nc.sync.dma_start(
+                    out=f_sb[0:C_TAIL, base + (NT - 1) * HW : base + NT * HW],
+                    in_=feat[b, (NT - 1) * P : C, :],
+                )
+
+            w_grouped = stage_w.tile([P, PASSES, INC, PACK], BF16, align_bytes=64)
+            for c in range(PASSES):
+                nc.vector.tensor_copy(
+                    out=w_grouped[:, c], in_=w_raw[:, c].rearrange("p j i -> p i j")
+                )
+            for c in range(PASSES):
+                nc.vector.quantize_mx(
+                    out=w_codes[:, c, :].bitcast(E4M3X4),
+                    scales=w_scales[:, c, :],
+                    in_=w_grouped[:, c].rearrange("p i j -> p (i j)"),
+                )
+
+            def masked_gradient(b, c):
+                o_rows = slice(c * K_PASS, (c + 1) * K_PASS)
+                z_t = stage_z.tile([P, PACK, HW], F32, name="z_t")
+                nc.sync.dma_start(
+                    out=z_t[:], in_=z_in[b, o_rows, :].rearrange("(p j) x -> p j x", j=PACK)
+                )
+                g_t = stage_z.tile([P, PACK, HW], BF16, name="g_t")
+                nc.sync.dma_start(
+                    out=g_t[:], in_=g_in[b, o_rows, :].rearrange("(p j) x -> p j x", j=PACK)
+                )
+                dz_t = stage_z.tile([P, 2, WORDS, PACK], BF16, name="dz_t", align_bytes=64)
+                z_par = z_t[:].rearrange("p j (m e) -> p e m j", e=2)
+                g_par = g_t[:].rearrange("p j (m e) -> p e m j", e=2)
+                for e in range(2):
+                    nc.vector.scalar_tensor_tensor(
+                        out=dz_t[:, e],
+                        in0=z_par[:, e],
+                        scalar=0.0,
+                        in1=g_par[:, e],
+                        op0=ALU.is_gt,
+                        op1=ALU.mult,
+                    )
+                return dz_t
+
+            def quantise_gradient(dz_t, b, c):
+                nc.vector.quantize_mx(
+                    out=dz_codes[:, b, c, :].bitcast(E5M2X4),
+                    scales=dz_scales[:, b, c, :],
+                    in_=dz_t[:].rearrange("p e m j -> p (e m j)"),
+                )
+
+            chunks = [(b, c) for b in range(B) for c in range(PASSES)]
+            masked = []
+            for i, (b, c) in enumerate(chunks):
+                masked.append(masked_gradient(b, c))
+                if i > 0:
+                    quantise_gradient(masked[i - 1], chunks[i - 1][0], chunks[i - 1][1])
+            quantise_gradient(masked[-1], chunks[-1][0], chunks[-1][1])
+
+        small = ctx.enter_context(tc.tile_pool(name="small", bufs=3))
+        scrap_pool = ctx.enter_context(tc.tile_pool(name="scrap", bufs=2))
+
+        for b in range(B):
+            tiles = slice(b * 2 * GROUPS, (b + 1) * 2 * GROUPS)
+            for d in range(GROUPS):
+                g = b * GROUPS + d
+                for half in range(2):
+                    bank = word_window(psum_v, g, 0, 0, half)
+                    nc.vector.tensor_copy(
+                        out=f_own[:, g, half * 2 * HALF : (half + 1) * 2 * HALF].bitcast(F32),
+                        in_=bank[:],
+                    )
+                    for e in range(2):
+                        squares = scrap_pool.tile([P, HALF], F32, name="squares")
+                        nc.scalar.activation(
+                            out=squares[:],
+                            in_=pixel_of_words(bank[:], e, HALF),
+                            func=ACT.Square,
+                            accum_out=sq_half[:, 2 * g + e, half : half + 1],
+                        )
+                for e in range(2):
+                    bank = psum_mx.tile([P, HALF], F32, tag="dx", name="dx")
+                    dx_group(g, e, 1, bank)
+                    nc.scalar.copy(out=own[:, 2 * g + e, :], in_=bank[:, HALF - P : HALF])
+
+            nc.vector.tensor_reduce(out=sq[:, tiles], in_=sq_half[:, tiles, :], axis=AX.X, op=ALU.add)
+            nc.vector.tensor_scalar_max(out=sq_floor[:, tiles], in0=sq[:, tiles], scalar1=EPS * EPS)
+            nc.scalar.activation(out=norm[:, tiles], in_=sq_floor[:, tiles], func=ACT.Sqrt)
+            nc.vector.reciprocal(out=rn[:, tiles], in_=norm[:, tiles])
+            nc.vector.tensor_tensor(out=rn2[:, tiles], in0=rn[:, tiles], in1=rn[:, tiles], op=ALU.mult)
+            nc.vector.tensor_scalar_mul(out=neg_rn2[:, tiles], in0=rn2[:, tiles], scalar1=-1.0)
+            nc.vector.tensor_tensor(
+                out=off_unit[:, tiles], in0=neg_rn2[:, tiles], in1=sq[:, tiles], op=ALU.mult
+            )
+            nc.vector.tensor_scalar_add(out=off_unit[:, tiles], in0=off_unit[:, tiles], scalar1=1.0)
+            nc.vector.tensor_copy(out=own[:, tiles, RN_ROW], in_=rn[:, tiles])
+
+            for e in range(2):
+                flipped = psum_o.tile([P, GROUPS, P], F32, tag="o", name="flipped")
+                for d in range(GROUPS):
+                    nc.tensor.transpose(
+                        out=flipped[:, d, :],
+                        in_=own[:, 2 * (b * GROUPS + d) + e, :],
+                        identity=ident[:],
+                    )
+                nc.scalar.copy(
+                    out=rows[:, b, e, R_PAD : R_PAD + WORDS],
+                    in_=flipped[:].rearrange("p d m -> p (d m)"),
+                )
+
+        acc_pool = ctx.enter_context(tc.tile_pool(name="acc", bufs=3))
+        prod_pool = ctx.enter_context(tc.tile_pool(name="prod", bufs=4))
+        fin_pool = ctx.enter_context(tc.tile_pool(name="fin", bufs=2))
+        accs = {}
+        gammas = {}
+        live = {}
+
+        def width_of(half):
+            return HALF if half == 0 else C - HALF
+
+        def coeff_step(g, e, r):
+            b, d = divmod(g, GROUPS)
+            ti = 2 * g + e
+            if r == 0:
+                live["there"] = psum_c.tile([P, NK, 2], F32, tag="there", name="there")
+            there = live["there"]
+            for cc in range(CS):
+                k = cc * CS + r
+                wsh, ep = divmod(e + cc - PAD, 2)
+                h0 = R_PAD + P * d + wsh + ROW_WORDS * (r - PAD)
+                nc.tensor.matmul(
+                    out=there[:, k, :],
+                    lhsT=rows[:, b, ep, h0 : h0 + P],
+                    rhs=ident[:, RN_ROW : P - k : NK - k],
+                    start=True,
+                    stop=True,
+                )
+            if r == CS - 1:
+                pair = small.tile([P, NK], F32, name="pair")
+                nc.vector.tensor_tensor(
+                    out=pair[:], in0=own[:, ti, C_TAIL:P], in1=there[:, :, 1], op=ALU.add
+                )
+                nc.vector.tensor_tensor(out=pair[:], in0=pair[:], in1=there[:, :, 0], op=ALU.mult)
+                nc.vector.scalar_tensor_tensor(
+                    out=alpha[:, ti, :],
+                    in0=pair[:],
+                    scalar=rn[:, ti : ti + 1],
+                    in1=in_row[:, e, :],
+                    op0=ALU.mult,
+                    op1=ALU.mult,
+                )
+                nc.vector.tensor_tensor(
+                    out=centre[:, ti : ti + 1],
+                    in0=alpha[:, ti, CENTRE : CENTRE + 1],
+                    in1=off_unit[:, ti : ti + 1],
+                    op=ALU.mult,
+                )
+
+        def pool_step(g, half, dy):
+            if half == 0 and dy == -PAD:
+                accs[g] = [
+                    acc_pool.tile([P, INC], F32, tag="acc%d" % e, name="acc%d" % e) for e in range(2)
+                ]
+            acc = accs[g]
+            width = width_of(half)
+            bank = word_window(psum_s, g, dy, 0, half)
+            for e in range(2):
+                for ep in range(2):
+                    dx = ep - e
+                    if dy == 0 and dx == 0:
+                        continue
+                    k = (dx + PAD) * CS + dy + PAD
+                    coeff = alpha[:, 2 * g + e, k : k + 1]
+                    if dy == -PAD and ep == 0:
+                        nc.scalar.activation(
+                            out=acc[e][:, half * HALF : (half + 1) * HALF],
+                            in_=pixel_of_words(bank[:], ep, HALF),
+                            func=ACT.Copy,
+                            scale=coeff,
+                        )
+                    else:
+                        prod = prod_pool.tile([P, HALF], F32, name="prod")
+                        nc.scalar.activation(
+                            out=prod[:, 0:width],
+                            in_=pixel_of_words(bank[:], ep, width),
+                            func=ACT.Copy,
+                            scale=coeff,
+                        )
+                        nc.gpsimd.tensor_tensor(
+                            out=acc[e][:, half * HALF : half * HALF + width],
+                            in0=acc[e][:, half * HALF : half * HALF + width],
+                            in1=prod[:, 0:width],
+                            op=ALU.add,
+                        )
+
+        def vector_step(g, half, dy):
+            acc = accs[g]
+            width = width_of(half)
+            for wsh in (-1, 1):
+                bank = word_window(psum_v, g, dy, wsh, half)
+                for e in range(2):
+                    for ep in range(2):
+                        dx = 2 * wsh + ep - e
+                        if abs(dx) > PAD:
+                            continue
+                        k = (dx + PAD) * CS + dy + PAD
+                        nc.vector.scalar_tensor_tensor(
+                            out=acc[e][:, half * HALF : half * HALF + width],
+                            in0=pixel_of_words(bank[:], ep, width),
+                            scalar=alpha[:, 2 * g + e, k : k + 1],
+                            in1=acc[e][:, half * HALF : half * HALF + width],
+                            op0=ALU.mult,
+                            op1=ALU.add,
+                        )
+
+        def own_feature(g, half, e, width):
+            words = f_own[:, g, half * 2 * HALF : (half + 1) * 2 * HALF].bitcast(F32)
+            return pixel_of_words(words, e, width)
+
+        def project(g):
+            acc = accs[g]
+            dots = small.tile([P, 2, 2], F32, name="dots")
+            for e in range(2):
+                for half in range(2):
+                    width = width_of(half)
+                    scrap = scrap_pool.tile([P, HALF], F32, name="scrap")
+                    nc.vector.scalar_tensor_tensor(
+                        out=scrap[:, 0:width],
+                        in0=own_feature(g, half, e, width),
+                        scalar=1.0,
+                        in1=acc[e][:, half * HALF : half * HALF + width],
+                        op0=ALU.mult,
+                        op1=ALU.mult,
+                        accum_out=dots[:, e, half : half + 1],
+                    )
+            dot = small.tile([P, 2], F32, name="dot")
+            nc.vector.tensor_reduce(out=dot[:], in_=dots[:], axis=AX.X, op=ALU.add)
+            gamma = small.tile([P, 2], F32, name="gamma")
+            nc.vector.tensor_tensor(
+                out=gamma[:], in0=dot[:], in1=neg_rn2[:, 2 * g : 2 * g + 2], op=ALU.mult
+            )
+            nc.vector.tensor_tensor(
+                out=gamma[:], in0=gamma[:], in1=centre[:, 2 * g : 2 * g + 2], op=ALU.add
+            )
+            gammas[g] = gamma
+
+        def finish_step(g, half, j):
+            b, d = divmod(g, GROUPS)
+            lo = half * HALF
+            if j < 2:
+                e = j
+                along = fin_pool.tile([P, HALF], F32, tag="along%d" % e, name="along%d" % e)
+                nc.scalar.activation(
+                    out=along[:],
+                    in_=own_feature(g, half, e, HALF),
+                    func=ACT.Copy,
+                    scale=gammas[g][:, e : e + 1],
+                )
+                bank = psum_mx.tile([P, HALF], F32, tag="dx", name="dx")
+                dx_group(g, e, half, bank)
+                dx_sb = fin_pool.tile([P, HALF], F32, tag="dx_sb%d" % e, name="dx_sb%d" % e)
+                nc.scalar.copy(out=dx_sb[:], in_=bank[:])
+                live[("parts", e)] = (accs[g][e][:, lo : lo + HALF], dx_sb[:], along[:])
+            elif j < 4:
+                if j == 2:
+                    live["o_sb"] = fin_pool.tile([P, HALF // P, 2 * P], F32, tag="o_sb", name="o_sb")
+                o_sb = live["o_sb"]
+                first = 2 * (j - 2)
+                o_ps = psum_o.tile([P, 2, 2, P], F32, tag="o", name="o_ps")
+                for t2 in range(2):
+                    t_cols = slice((first + t2) * P, (first + t2 + 1) * P)
+                    for e in range(2):
+                        parts = live[("parts", e)]
+                        for i, part in enumerate(parts):
+                            nc.tensor.matmul(
+                                out=o_ps[:, t2, e, :],
+                                lhsT=part[:, t_cols],
+                                rhs=ident[:],
+                                is_transpose=True,
+                                start=(i == 0),
+                                stop=(i == len(parts) - 1),
+                            )
+                nc.scalar.copy(
+                    out=o_sb[:, first : first + 2, :].rearrange("p t (m e) -> p t m e", e=2),
+                    in_=o_ps[:].rearrange("p t e m -> p t m e"),
+                )
+            else:
+                o_sb = live["o_sb"]
+                px = slice(2 * P * d, 2 * P * (d + 1))
+                whole = HALF // P if half == 0 else HALF // P - 1
+                nc.sync.dma_start(
+                    out=res[b, lo : lo + whole * P, px].rearrange("(t p) x -> p t x", p=P),
+                    in_=o_sb[:, 0:whole, :],
+                )
+                if half == 1:
+                    nc.sync.dma_start(out=res[b, lo + whole * P : C, px], in_=o_sb[0:C_TAIL, whole, :])
+
+        for g in range(-2, NG + 1):
+            for a in range(2):
+                for r in range(CS):
+                    if 0 <= g + 2 < NG:
+                        coeff_step(g + 2, a, r)
+                    if 0 <= g + 1 < NG:
+                        pool_step(g + 1, a, r - PAD)
+                    if 0 <= g < NG:
+                        vector_step(g, a, r - PAD)
+                    if 0 <= g - 1 < NG:
+                        finish_step(g - 1, a, r)
+            if 0 <= g < NG:
+                project(g)

@@ -310,8 +310,8 @@ def tile_spatialcontext_t_v_kernel(tc, feature, conv_w, conv_b, z, grad_out, out
             acc = accs[g]
             width = width_of(half)
             bank = word_window(psum_s, g, dy, 0, half)
-            for e in range(2):
-                for ep in range(2):
+            for ep in range(2):
+                for e in range(2):
                     dx = ep - e
                     if dy == 0 and dx == 0:
                         continue
@@ -342,22 +342,25 @@ def tile_spatialcontext_t_v_kernel(tc, feature, conv_w, conv_b, z, grad_out, out
         def vector_step(g, half, dy):
             acc = accs[g]
             width = width_of(half)
+            terms = ([], [])
             for wsh in (-1, 1):
                 bank = word_window(psum_v, g, dy, wsh, half)
-                for e in range(2):
-                    for ep in range(2):
+                for ep in range(2):
+                    for e in range(2):
                         dx = 2 * wsh + ep - e
-                        if abs(dx) > PAD:
-                            continue
-                        k = (dx + PAD) * CS + dy + PAD
-                        nc.vector.scalar_tensor_tensor(
-                            out=acc[e][:, half * HALF : half * HALF + width],
-                            in0=pixel_of_words(bank[:], ep, width),
-                            scalar=alpha[:, 2 * g + e, k : k + 1],
-                            in1=acc[e][:, half * HALF : half * HALF + width],
-                            op0=ALU.mult,
-                            op1=ALU.add,
-                        )
+                        if abs(dx) <= PAD:
+                            terms[e].append((bank, ep, (dx + PAD) * CS + dy + PAD))
+            for turn in zip(terms[0], terms[1]):
+                for e in range(2):
+                    bank, ep, k = turn[e]
+                    nc.vector.scalar_tensor_tensor(
+                        out=acc[e][:, half * HALF : half * HALF + width],
+                        in0=pixel_of_words(bank[:], ep, width),
+                        scalar=alpha[:, 2 * g + e, k : k + 1],
+                        in1=acc[e][:, half * HALF : half * HALF + width],
+                        op0=ALU.mult,
+                        op1=ALU.add,
+                    )
 
         def own_feature(g, half, e, width):
             words = f_own[:, g, half * 2 * HALF : (half + 1) * 2 * HALF].bitcast(F32)
@@ -441,16 +444,17 @@ def tile_spatialcontext_t_v_kernel(tc, feature, conv_w, conv_b, z, grad_out, out
                 if half == 1:
                     nc.sync.dma_start(out=res[b, lo + whole * P : C, px], in_=o_sb[0:C_TAIL, whole, :])
 
-        for g in range(-2, NG + 1):
-            for a in range(2):
-                for r in range(CS):
-                    if 0 <= g + 2 < NG:
-                        coeff_step(g + 2, a, r)
-                    if 0 <= g + 1 < NG:
-                        pool_step(g + 1, a, r - PAD)
-                    if 0 <= g < NG:
-                        vector_step(g, a, r - PAD)
-                    if 0 <= g - 1 < NG:
-                        finish_step(g - 1, a, r)
-            if 0 <= g < NG:
-                project(g)
+        with tc.manual_schedule():
+            for g in range(-2, NG + 1):
+                for a in range(2):
+                    for r in range(CS):
+                        if 0 <= g + 2 < NG:
+                            coeff_step(g + 2, a, r)
+                        if 0 <= g + 1 < NG:
+                            pool_step(g + 1, a, r - PAD)
+                        if 0 <= g < NG:
+                            vector_step(g, a, r - PAD)
+                        if 0 <= g - 1 < NG:
+                            finish_step(g - 1, a, r)
+                if 0 <= g < NG:
+                    project(g)

@@ -35,6 +35,7 @@ HALF = 512
 F_PAD = 128
 R_PAD = 64
 RN_ROW = C_TAIL - 1
+EARLY = 2
 
 FLOPS = 2 * OC * INC * B * HW + 4 * NK * C * B * HW
 
@@ -89,8 +90,8 @@ def tile_spatialcontext_t_v_kernel(tc, feature, conv_w, conv_b, z, grad_out, out
 
         w_codes = keep.tile([P, PASSES, INC], U32, align_bytes=64)
         w_scales = keep.tile([P, PASSES, INC], U8, align_bytes=64)
-        dz_codes = keep.tile([P, B, PASSES, HW], U32, align_bytes=64)
-        dz_scales = keep.tile([P, B, PASSES, HW], U8, align_bytes=64)
+        dz_codes = keep.tile([P, NG, PASSES, 2 * P], U32, align_bytes=64)
+        dz_scales = keep.tile([P, NG, PASSES, 2 * P], U8, align_bytes=64)
         own = keep.tile([P, 2 * NG, P], F32)
         rows = keep.tile([P, B, 2, 2 * R_PAD + WORDS], F32)
         nc.gpsimd.memset(rows[:], 0.0)
@@ -105,6 +106,44 @@ def tile_spatialcontext_t_v_kernel(tc, feature, conv_w, conv_b, z, grad_out, out
         neg_rn2 = keep.tile([P, 2 * NG], F32)
         off_unit = keep.tile([P, 2 * NG], F32)
         centre = keep.tile([P, 2 * NG], F32)
+
+        stage_z = ctx.enter_context(tc.tile_pool(name="stage_z", bufs=2))
+
+        with tc.tile_pool(name="stage_w", bufs=1) as stage_w:
+            w_raw = stage_w.tile([P, PASSES, PACK, INC], BF16)
+            nc.sync.dma_start(
+                out=w_raw[:], in_=conv_w.rearrange("(c p j) i -> p c j i", p=P, j=PACK)
+            )
+            for b in range(B):
+                base = F_PAD + b * NT * HW
+                nc.sync.dma_start(
+                    out=f_sb[:, base : base + (NT - 1) * HW].rearrange("p (t x) -> p t x", x=HW),
+                    in_=feat[b, 0 : (NT - 1) * P, :].rearrange("(t p) x -> p t x", p=P),
+                )
+                nc.sync.dma_start(
+                    out=f_sb[0:C_TAIL, base + (NT - 1) * HW : base + NT * HW],
+                    in_=feat[b, (NT - 1) * P : C, :],
+                )
+            w_grouped = stage_w.tile([P, PASSES, INC, PACK], BF16, align_bytes=64)
+            for c in range(PASSES):
+                nc.vector.tensor_copy(
+                    out=w_grouped[:, c], in_=w_raw[:, c].rearrange("p j i -> p i j")
+                )
+            for c in range(PASSES):
+                nc.vector.quantize_mx(
+                    out=w_codes[:, c, :].bitcast(E4M3X4),
+                    scales=w_scales[:, c, :],
+                    in_=w_grouped[:, c].rearrange("p i j -> p (i j)"),
+                )
+
+        small = ctx.enter_context(tc.tile_pool(name="small", bufs=3))
+        scrap_pool = ctx.enter_context(tc.tile_pool(name="scrap", bufs=2))
+        acc_pool = ctx.enter_context(tc.tile_pool(name="acc", bufs=3))
+        prod_pool = ctx.enter_context(tc.tile_pool(name="prod", bufs=4))
+        fin_pool = ctx.enter_context(tc.tile_pool(name="fin", bufs=2))
+        accs = {}
+        gammas = {}
+        live = {}
 
         def word_window(pool, g, dy, wsh, half):
             b, d = divmod(g, GROUPS)
@@ -121,148 +160,124 @@ def tile_spatialcontext_t_v_kernel(tc, feature, conv_w, conv_b, z, grad_out, out
             return words.bitcast(BF16).rearrange("p (c e) -> p c e", e=2)[:, 0:width, ep]
 
         def dx_group(g, e, half, bank):
-            b, d = divmod(g, GROUPS)
-            cols = slice(e * WORDS + d * P, e * WORDS + (d + 1) * P)
+            cols = slice(e * P, (e + 1) * P)
             for c in range(PASSES):
                 nc.tensor.matmul_mx(
                     out=bank[:],
-                    lhsT=dz_codes[:, b, c, cols].bitcast(E5M2X4),
-                    lhsT_scale=dz_scales[:, b, c, cols],
+                    lhsT=dz_codes[:, g, c, cols].bitcast(E5M2X4),
+                    lhsT_scale=dz_scales[:, g, c, cols],
                     rhs=w_codes[:, c, half * HALF : (half + 1) * HALF].bitcast(E4M3X4),
                     rhs_scale=w_scales[:, c, half * HALF : (half + 1) * HALF],
                     start=(c == 0),
                     stop=(c == PASSES - 1),
                 )
 
-        with tc.tile_pool(name="stage_w", bufs=1) as stage_w, tc.tile_pool(
-            name="stage_z", bufs=2
-        ) as stage_z:
-            w_raw = stage_w.tile([P, PASSES, PACK, INC], BF16)
-            nc.sync.dma_start(
-                out=w_raw[:], in_=conv_w.rearrange("(c p j) i -> p c j i", p=P, j=PACK)
-            )
-            for b in range(B):
-                base = F_PAD + b * NT * HW
-                nc.sync.dma_start(
-                    out=f_sb[:, base : base + (NT - 1) * HW].rearrange("p (t x) -> p t x", x=HW),
-                    in_=feat[b, 0 : (NT - 1) * P, :].rearrange("(t p) x -> p t x", p=P),
-                )
-                nc.sync.dma_start(
-                    out=f_sb[0:C_TAIL, base + (NT - 1) * HW : base + NT * HW],
-                    in_=feat[b, (NT - 1) * P : C, :],
-                )
+        def width_of(half):
+            return HALF if half == 0 else C - HALF
 
-            w_grouped = stage_w.tile([P, PASSES, INC, PACK], BF16, align_bytes=64)
+        def load_gradient(g):
+            b, d = divmod(g, GROUPS)
+            px = slice(2 * P * d, 2 * P * (d + 1))
+            z_t = stage_z.tile([P, PASSES, PACK, 2 * P], F32, name="z_t")
+            g_t = stage_z.tile([P, PASSES, PACK, 2 * P], BF16, name="g_t")
             for c in range(PASSES):
-                nc.vector.tensor_copy(
-                    out=w_grouped[:, c], in_=w_raw[:, c].rearrange("p j i -> p i j")
-                )
-            for c in range(PASSES):
-                nc.vector.quantize_mx(
-                    out=w_codes[:, c, :].bitcast(E4M3X4),
-                    scales=w_scales[:, c, :],
-                    in_=w_grouped[:, c].rearrange("p i j -> p (i j)"),
-                )
-
-            def masked_gradient(b, c):
                 o_rows = slice(c * K_PASS, (c + 1) * K_PASS)
-                z_t = stage_z.tile([P, PACK, HW], F32, name="z_t")
                 nc.sync.dma_start(
-                    out=z_t[:], in_=z_in[b, o_rows, :].rearrange("(p j) x -> p j x", j=PACK)
+                    out=z_t[:, c], in_=z_in[b, o_rows, px].rearrange("(p j) x -> p j x", j=PACK)
                 )
-                g_t = stage_z.tile([P, PACK, HW], BF16, name="g_t")
                 nc.sync.dma_start(
-                    out=g_t[:], in_=g_in[b, o_rows, :].rearrange("(p j) x -> p j x", j=PACK)
+                    out=g_t[:, c], in_=g_in[b, o_rows, px].rearrange("(p j) x -> p j x", j=PACK)
                 )
-                dz_t = stage_z.tile([P, 2, WORDS, PACK], BF16, name="dz_t", align_bytes=64)
-                z_par = z_t[:].rearrange("p j (m e) -> p e m j", e=2)
-                g_par = g_t[:].rearrange("p j (m e) -> p e m j", e=2)
+            live[("z", g)] = z_t
+            live[("g", g)] = g_t
+
+        def mask_gradient(g):
+            dz_t = stage_z.tile([P, PASSES, 2, P, PACK], BF16, name="dz_t", align_bytes=64)
+            for c in range(PASSES):
+                z_par = live[("z", g)][:, c].rearrange("p j (m e) -> p e m j", e=2)
+                g_par = live[("g", g)][:, c].rearrange("p j (m e) -> p e m j", e=2)
                 for e in range(2):
                     nc.vector.scalar_tensor_tensor(
-                        out=dz_t[:, e],
+                        out=dz_t[:, c, e],
                         in0=z_par[:, e],
                         scalar=0.0,
                         in1=g_par[:, e],
                         op0=ALU.is_gt,
                         op1=ALU.mult,
                     )
-                return dz_t
+            live[("dz", g)] = dz_t
 
-            def quantise_gradient(dz_t, b, c):
+        def quantise_gradient(g):
+            for c in range(PASSES):
                 nc.vector.quantize_mx(
-                    out=dz_codes[:, b, c, :].bitcast(E5M2X4),
-                    scales=dz_scales[:, b, c, :],
-                    in_=dz_t[:].rearrange("p e m j -> p (e m j)"),
+                    out=dz_codes[:, g, c, :].bitcast(E5M2X4),
+                    scales=dz_scales[:, g, c, :],
+                    in_=live[("dz", g)][:, c].rearrange("p e m j -> p (e m j)"),
                 )
 
-            chunks = [(b, c) for b in range(B) for c in range(PASSES)]
-            masked = []
-            for i, (b, c) in enumerate(chunks):
-                masked.append(masked_gradient(b, c))
-                if i > 0:
-                    quantise_gradient(masked[i - 1], chunks[i - 1][0], chunks[i - 1][1])
-            quantise_gradient(masked[-1], chunks[-1][0], chunks[-1][1])
-
-        small = ctx.enter_context(tc.tile_pool(name="small", bufs=3))
-        scrap_pool = ctx.enter_context(tc.tile_pool(name="scrap", bufs=2))
-
-        for b in range(B):
-            tiles = slice(b * 2 * GROUPS, (b + 1) * 2 * GROUPS)
-            for d in range(GROUPS):
-                g = b * GROUPS + d
-                for half in range(2):
-                    bank = word_window(psum_v, g, 0, 0, half)
-                    nc.vector.tensor_copy(
-                        out=f_own[:, g, half * 2 * HALF : (half + 1) * 2 * HALF].bitcast(F32),
-                        in_=bank[:],
-                    )
-                    for e in range(2):
-                        squares = scrap_pool.tile([P, HALF], F32, name="squares")
-                        nc.scalar.activation(
-                            out=squares[:],
-                            in_=pixel_of_words(bank[:], e, HALF),
-                            func=ACT.Square,
-                            accum_out=sq_half[:, 2 * g + e, half : half + 1],
-                        )
-                for e in range(2):
-                    bank = psum_mx.tile([P, HALF], F32, tag="dx", name="dx")
-                    dx_group(g, e, 1, bank)
-                    nc.scalar.copy(out=own[:, 2 * g + e, :], in_=bank[:, HALF - P : HALF])
-
-            nc.vector.tensor_reduce(out=sq[:, tiles], in_=sq_half[:, tiles, :], axis=AX.X, op=ALU.add)
-            nc.vector.tensor_scalar_max(out=sq_floor[:, tiles], in0=sq[:, tiles], scalar1=EPS * EPS)
-            nc.scalar.activation(out=norm[:, tiles], in_=sq_floor[:, tiles], func=ACT.Sqrt)
-            nc.vector.reciprocal(out=rn[:, tiles], in_=norm[:, tiles])
-            nc.vector.tensor_tensor(out=rn2[:, tiles], in0=rn[:, tiles], in1=rn[:, tiles], op=ALU.mult)
-            nc.vector.tensor_scalar_mul(out=neg_rn2[:, tiles], in0=rn2[:, tiles], scalar1=-1.0)
-            nc.vector.tensor_tensor(
-                out=off_unit[:, tiles], in0=neg_rn2[:, tiles], in1=sq[:, tiles], op=ALU.mult
+        def own_features(g, half):
+            bank = word_window(psum_s, g, 0, 0, half)
+            nc.scalar.copy(
+                out=f_own[:, g, half * 2 * HALF : (half + 1) * 2 * HALF], in_=bank[:].bitcast(BF16)
             )
-            nc.vector.tensor_scalar_add(out=off_unit[:, tiles], in0=off_unit[:, tiles], scalar1=1.0)
-            nc.vector.tensor_copy(out=own[:, tiles, RN_ROW], in_=rn[:, tiles])
-
             for e in range(2):
-                flipped = psum_o.tile([P, GROUPS, P], F32, tag="o", name="flipped")
-                for d in range(GROUPS):
-                    nc.tensor.transpose(
-                        out=flipped[:, d, :],
-                        in_=own[:, 2 * (b * GROUPS + d) + e, :],
-                        identity=ident[:],
-                    )
-                nc.scalar.copy(
-                    out=rows[:, b, e, R_PAD : R_PAD + WORDS],
-                    in_=flipped[:].rearrange("p d m -> p (d m)"),
+                squares = scrap_pool.tile([P, HALF], F32, name="squares")
+                nc.scalar.activation(
+                    out=squares[:],
+                    in_=pixel_of_words(bank[:], e, HALF),
+                    func=ACT.Square,
+                    accum_out=sq_half[:, 2 * g + e, half : half + 1],
                 )
 
-        acc_pool = ctx.enter_context(tc.tile_pool(name="acc", bufs=3))
-        prod_pool = ctx.enter_context(tc.tile_pool(name="prod", bufs=4))
-        fin_pool = ctx.enter_context(tc.tile_pool(name="fin", bufs=2))
-        accs = {}
-        gammas = {}
-        live = {}
+        def own_dx(g, e):
+            bank = psum_mx.tile([P, HALF], F32, tag="dx", name="dx")
+            dx_group(g, e, 1, bank)
+            nc.scalar.copy(out=own[:, 2 * g + e, :], in_=bank[:, HALF - P : HALF])
 
-        def width_of(half):
-            return HALF if half == 0 else C - HALF
+        def norm_floor(g):
+            two = slice(2 * g, 2 * g + 2)
+            nc.vector.tensor_reduce(out=sq[:, two], in_=sq_half[:, two, :], axis=AX.X, op=ALU.add)
+            nc.vector.tensor_scalar_max(out=sq_floor[:, two], in0=sq[:, two], scalar1=EPS * EPS)
+
+        def norm_root(g):
+            two = slice(2 * g, 2 * g + 2)
+            nc.scalar.activation(out=norm[:, two], in_=sq_floor[:, two], func=ACT.Sqrt)
+
+        def norm_inverse(g):
+            two = slice(2 * g, 2 * g + 2)
+            nc.vector.reciprocal(out=rn[:, two], in_=norm[:, two])
+            nc.vector.tensor_copy(out=own[:, two, RN_ROW], in_=rn[:, two])
+            nc.vector.tensor_tensor(out=rn2[:, two], in0=rn[:, two], in1=rn[:, two], op=ALU.mult)
+            nc.vector.tensor_scalar_mul(out=neg_rn2[:, two], in0=rn2[:, two], scalar1=-1.0)
+            nc.vector.tensor_tensor(
+                out=off_unit[:, two], in0=neg_rn2[:, two], in1=sq[:, two], op=ALU.mult
+            )
+            nc.vector.tensor_scalar_add(out=off_unit[:, two], in0=off_unit[:, two], scalar1=1.0)
+
+        def flip_own(g):
+            b, d = divmod(g, GROUPS)
+            flipped = psum_o.tile([P, 2, P], F32, tag="o", name="flipped")
+            for e in range(2):
+                nc.tensor.transpose(out=flipped[:, e, :], in_=own[:, 2 * g + e, :], identity=ident[:])
+            nc.scalar.copy(out=rows[:, b, :, R_PAD + P * d : R_PAD + P * (d + 1)], in_=flipped[:])
+
+        def prepare_step(g, s):
+            if s == 0:
+                mask_gradient(g)
+            elif s == 1:
+                quantise_gradient(g)
+            elif s < 4:
+                own_features(g, s - 2)
+            elif s < 6:
+                own_dx(g, s - 4)
+            elif s == 6:
+                norm_floor(g)
+            elif s == 7:
+                norm_root(g)
+            elif s == 8:
+                norm_inverse(g)
+            else:
+                flip_own(g)
 
         def coeff_step(g, e, r):
             b, d = divmod(g, GROUPS)
@@ -270,18 +285,19 @@ def tile_spatialcontext_t_v_kernel(tc, feature, conv_w, conv_b, z, grad_out, out
             if r == 0:
                 live["there"] = psum_c.tile([P, NK, 2], F32, tag="there", name="there")
             there = live["there"]
-            for cc in range(CS):
-                k = cc * CS + r
-                wsh, ep = divmod(e + cc - PAD, 2)
-                h0 = R_PAD + P * d + wsh + ROW_WORDS * (r - PAD)
-                nc.tensor.matmul(
-                    out=there[:, k, :],
-                    lhsT=rows[:, b, ep, h0 : h0 + P],
-                    rhs=ident[:, RN_ROW : P - k : NK - k],
-                    start=True,
-                    stop=True,
-                )
-            if r == CS - 1:
+            if r < CS - 1:
+                for k in range(r, NK, CS - 1):
+                    dy, dx = k % CS - PAD, k // CS - PAD
+                    wsh, ep = divmod(e + dx, 2)
+                    h0 = R_PAD + P * d + wsh + ROW_WORDS * dy
+                    nc.tensor.matmul(
+                        out=there[:, k, :],
+                        lhsT=rows[:, b, ep, h0 : h0 + P],
+                        rhs=ident[:, RN_ROW : P - k : NK - k],
+                        start=True,
+                        stop=True,
+                    )
+            else:
                 pair = small.tile([P, NK], F32, name="pair")
                 nc.vector.tensor_tensor(
                     out=pair[:], in0=own[:, ti, C_TAIL:P], in1=there[:, :, 1], op=ALU.add
@@ -302,20 +318,22 @@ def tile_spatialcontext_t_v_kernel(tc, feature, conv_w, conv_b, z, grad_out, out
                     op=ALU.mult,
                 )
 
+        def middle_on_pool(g, dy):
+            return dy == -PAD or (g > 0 and dy != 0)
+
         def pool_step(g, half, dy):
             if half == 0 and dy == -PAD:
                 accs[g] = [
                     acc_pool.tile([P, INC], F32, tag="acc%d" % e, name="acc%d" % e) for e in range(2)
                 ]
+            if not middle_on_pool(g, dy):
+                return
             acc = accs[g]
             width = width_of(half)
             bank = word_window(psum_s, g, dy, 0, half)
             for ep in range(2):
                 for e in range(2):
-                    dx = ep - e
-                    if dy == 0 and dx == 0:
-                        continue
-                    k = (dx + PAD) * CS + dy + PAD
+                    k = (ep - e + PAD) * CS + dy + PAD
                     coeff = alpha[:, 2 * g + e, k : k + 1]
                     if dy == -PAD and ep == 0:
                         nc.scalar.activation(
@@ -343,12 +361,14 @@ def tile_spatialcontext_t_v_kernel(tc, feature, conv_w, conv_b, z, grad_out, out
             acc = accs[g]
             width = width_of(half)
             terms = ([], [])
-            for wsh in (-1, 1):
+            for wsh in (-1, 0, 1):
+                if wsh == 0 and middle_on_pool(g, dy):
+                    continue
                 bank = word_window(psum_v, g, dy, wsh, half)
                 for ep in range(2):
                     for e in range(2):
                         dx = 2 * wsh + ep - e
-                        if abs(dx) <= PAD:
+                        if abs(dx) <= PAD and (dx != 0 or dy != 0):
                             terms[e].append((bank, ep, (dx + PAD) * CS + dy + PAD))
             for turn in zip(terms[0], terms[1]):
                 for e in range(2):
@@ -445,16 +465,26 @@ def tile_spatialcontext_t_v_kernel(tc, feature, conv_w, conv_b, z, grad_out, out
                     nc.sync.dma_start(out=res[b, lo + whole * P : C, px], in_=o_sb[0:C_TAIL, whole, :])
 
         with tc.manual_schedule():
-            for g in range(-2, NG + 1):
+            for g in range(EARLY):
+                load_gradient(g)
+            for s in range(2 * CS):
+                for g in range(EARLY):
+                    prepare_step(g, s)
+            load_gradient(EARLY)
+            for i in range(-2, NG + 1):
+                if EARLY < i + 5 < NG:
+                    load_gradient(i + 5)
                 for a in range(2):
                     for r in range(CS):
-                        if 0 <= g + 2 < NG:
-                            coeff_step(g + 2, a, r)
-                        if 0 <= g + 1 < NG:
-                            pool_step(g + 1, a, r - PAD)
-                        if 0 <= g < NG:
-                            vector_step(g, a, r - PAD)
-                        if 0 <= g - 1 < NG:
-                            finish_step(g - 1, a, r)
-                if 0 <= g < NG:
-                    project(g)
+                        if EARLY <= i + 4 < NG:
+                            prepare_step(i + 4, a * CS + r)
+                        if 0 <= i + 2 < NG:
+                            coeff_step(i + 2, a, r)
+                        if 0 <= i + 1 < NG:
+                            pool_step(i + 1, a, r - PAD)
+                        if 0 <= i < NG:
+                            vector_step(i, a, r - PAD)
+                        if 0 <= i - 1 < NG:
+                            finish_step(i - 1, a, r)
+                if 0 <= i < NG:
+                    project(i)

@@ -33,8 +33,12 @@ GROUPS = WORDS // P
 NG = B * GROUPS
 HALF = 512
 F_PAD = 128
-R_PAD = 64
-RN_ROW = C_TAIL - 1
+OWN_W = 32
+DV0 = OWN_W - NK
+RN_COL = DV0 - 1
+MARGIN = 128
+SCR_CH = (HW + 2 * MARGIN) * OWN_W // HW
+THERE_W = 1024
 EARLY = 2
 
 FLOPS = 2 * OC * INC * B * HW + 4 * NK * C * B * HW
@@ -49,11 +53,10 @@ def tile_spatialcontext_t_v_kernel(tc, feature, conv_w, conv_b, z, grad_out, out
 
     with ExitStack() as ctx:
         keep = ctx.enter_context(tc.tile_pool(name="keep", bufs=1))
-        psum_v = ctx.enter_context(tc.psum_pool(name="psum_v", bufs=3))
+        psum_v = ctx.enter_context(tc.psum_pool(name="psum_v", bufs=4))
         psum_s = ctx.enter_context(tc.psum_pool(name="psum_s", bufs=2))
         psum_mx = ctx.enter_context(tc.psum_pool(name="psum_mx", bufs=1))
         psum_o = ctx.enter_context(tc.psum_pool(name="psum_o", bufs=1))
-        psum_c = ctx.enter_context(tc.psum_pool(name="psum_c", bufs=1))
 
         ident = keep.tile([P, P], F32)
         make_identity(nc, ident[:])
@@ -68,7 +71,7 @@ def tile_spatialcontext_t_v_kernel(tc, feature, conv_w, conv_b, z, grad_out, out
         nc.vector.tensor_scalar(
             out=inside[:], in0=at_edge[:], scalar1=-1.0, scalar2=1.0, op0=ALU.mult, op1=ALU.add
         )
-        in_row = keep.tile([P, 2, NK], F32)
+        in_row = keep.tile([P, 2, CS, CS], F32)
         nc.vector.memset(in_row[:], 1.0)
         for e in range(2):
             for cc in range(CS):
@@ -76,7 +79,7 @@ def tile_spatialcontext_t_v_kernel(tc, feature, conv_w, conv_b, z, grad_out, out
                 if wsh != 0:
                     side = 0 if wsh < 0 else 1
                     nc.vector.tensor_copy(
-                        out=in_row[:, e, CS * cc : CS * (cc + 1)],
+                        out=in_row[:, e, :, cc],
                         in_=inside[:, side : side + 1].to_broadcast([P, CS]),
                     )
 
@@ -92,9 +95,16 @@ def tile_spatialcontext_t_v_kernel(tc, feature, conv_w, conv_b, z, grad_out, out
         w_scales = keep.tile([P, PASSES, INC], U8, align_bytes=64)
         dz_codes = keep.tile([P, NG, PASSES, 2 * P], U32, align_bytes=64)
         dz_scales = keep.tile([P, NG, PASSES, 2 * P], U8, align_bytes=64)
-        own = keep.tile([P, 2 * NG, P], F32)
-        rows = keep.tile([P, B, 2, 2 * R_PAD + WORDS], F32)
-        nc.gpsimd.memset(rows[:], 0.0)
+        own = keep.tile([P, 2 * NG, OWN_W], F32)
+        scratch = [
+            out[B - 1, C - (B - b) * SCR_CH : C - (B - b - 1) * SCR_CH].rearrange("c h w -> (c h) w")
+            for b in range(B)
+        ]
+        zeros = keep.tile([P, OWN_W], F32)
+        nc.vector.memset(zeros[:], 0.0)
+        for b in range(B):
+            nc.sync.dma_start(out=scratch[b][0:MARGIN, :], in_=zeros[:])
+            nc.sync.dma_start(out=scratch[b][MARGIN + HW : 2 * MARGIN + HW, :], in_=zeros[:])
         f_own = keep.tile([P, NG, 2 * INC], BF16)
         alpha = keep.tile([P, 2 * NG, NK], F32)
         sq_half = keep.tile([P, 2 * NG, 2], F32)
@@ -141,6 +151,7 @@ def tile_spatialcontext_t_v_kernel(tc, feature, conv_w, conv_b, z, grad_out, out
         acc_pool = ctx.enter_context(tc.tile_pool(name="acc", bufs=3))
         prod_pool = ctx.enter_context(tc.tile_pool(name="prod", bufs=4))
         fin_pool = ctx.enter_context(tc.tile_pool(name="fin", bufs=2))
+        fetch_pool = ctx.enter_context(tc.tile_pool(name="fetch", bufs=2))
         accs = {}
         gammas = {}
         live = {}
@@ -232,7 +243,7 @@ def tile_spatialcontext_t_v_kernel(tc, feature, conv_w, conv_b, z, grad_out, out
         def own_dx(g, e):
             bank = psum_mx.tile([P, HALF], F32, tag="dx", name="dx")
             dx_group(g, e, 1, bank)
-            nc.scalar.copy(out=own[:, 2 * g + e, :], in_=bank[:, HALF - P : HALF])
+            nc.scalar.copy(out=own[:, 2 * g + e, :], in_=bank[:, HALF - OWN_W : HALF])
 
         def norm_floor(g):
             two = slice(2 * g, 2 * g + 2)
@@ -246,7 +257,7 @@ def tile_spatialcontext_t_v_kernel(tc, feature, conv_w, conv_b, z, grad_out, out
         def norm_inverse(g):
             two = slice(2 * g, 2 * g + 2)
             nc.vector.reciprocal(out=rn[:, two], in_=norm[:, two])
-            nc.vector.tensor_copy(out=own[:, two, RN_ROW], in_=rn[:, two])
+            nc.vector.tensor_copy(out=own[:, two, RN_COL], in_=rn[:, two])
             nc.vector.tensor_tensor(out=rn2[:, two], in0=rn[:, two], in1=rn[:, two], op=ALU.mult)
             nc.vector.tensor_scalar_mul(out=neg_rn2[:, two], in0=rn2[:, two], scalar1=-1.0)
             nc.vector.tensor_tensor(
@@ -254,12 +265,13 @@ def tile_spatialcontext_t_v_kernel(tc, feature, conv_w, conv_b, z, grad_out, out
             )
             nc.vector.tensor_scalar_add(out=off_unit[:, two], in0=off_unit[:, two], scalar1=1.0)
 
-        def flip_own(g):
+        def store_own(g):
             b, d = divmod(g, GROUPS)
-            flipped = psum_o.tile([P, 2, P], F32, tag="o", name="flipped")
-            for e in range(2):
-                nc.tensor.transpose(out=flipped[:, e, :], in_=own[:, 2 * g + e, :], identity=ident[:])
-            nc.scalar.copy(out=rows[:, b, :, R_PAD + P * d : R_PAD + P * (d + 1)], in_=flipped[:])
+            first = MARGIN + 2 * P * d
+            nc.sync.dma_start(
+                out=scratch[b][first : first + 2 * P, :].rearrange("(m e) w -> m e w", e=2),
+                in_=own[:, 2 * g : 2 * g + 2, :],
+            )
 
         def prepare_step(g, s):
             if s == 0:
@@ -277,37 +289,45 @@ def tile_spatialcontext_t_v_kernel(tc, feature, conv_w, conv_b, z, grad_out, out
             elif s == 8:
                 norm_inverse(g)
             else:
-                flip_own(g)
+                store_own(g)
 
         def coeff_step(g, e, r):
             b, d = divmod(g, GROUPS)
             ti = 2 * g + e
-            if r == 0:
-                live["there"] = psum_c.tile([P, NK, 2], F32, tag="there", name="there")
-            there = live["there"]
-            if r < CS - 1:
-                for k in range(r, NK, CS - 1):
-                    dy, dx = k % CS - PAD, k // CS - PAD
-                    wsh, ep = divmod(e + dx, 2)
-                    h0 = R_PAD + P * d + wsh + ROW_WORDS * dy
-                    nc.tensor.matmul(
-                        out=there[:, k, :],
-                        lhsT=rows[:, b, ep, h0 : h0 + P],
-                        rhs=ident[:, RN_ROW : P - k : NK - k],
-                        start=True,
-                        stop=True,
-                    )
-            else:
-                pair = small.tile([P, NK], F32, name="pair")
+            if e == 0 and r == 0:
+                there = fetch_pool.tile([P, THERE_W], F32, name="there")
+                slots = there[:, 0 : CS * 6 * OWN_W].rearrange("p (r j w) -> p r j w", r=CS, j=6)
+                for rr in range(CS):
+                    for wsh in (-1, 0, 1):
+                        first = MARGIN + 2 * P * d + 2 * wsh + 2 * ROW_WORDS * (rr - PAD)
+                        nc.sync.dma_start(
+                            out=slots[:, rr, 2 * (wsh + 1) : 2 * (wsh + 2), :],
+                            in_=scratch[b][first : first + 2 * P, :].rearrange("(m e) w -> m e w", e=2),
+                        )
+                live["there"] = there
+            if r == CS - 1:
+                there = live["there"]
+                slots = there[:, 0 : CS * 6 * OWN_W].rearrange("p (r j w) -> p r j w", r=CS, j=6)
+                start = e * OWN_W + OWN_W - 1
+                row_step, col_step = 6 * OWN_W - 1, OWN_W - CS
+                partner = there[:, start : start + CS * row_step].rearrange(
+                    "p (r x) -> p r x", x=row_step
+                )[:, :, 0 : (CS - 1) * col_step + 1 : col_step]
+                pair = small.tile([P, CS, CS], F32, name="pair")
                 nc.vector.tensor_tensor(
-                    out=pair[:], in0=own[:, ti, C_TAIL:P], in1=there[:, :, 1], op=ALU.add
+                    out=pair[:],
+                    in0=own[:, ti, DV0:OWN_W].rearrange("p (cc r) -> p r cc", r=CS),
+                    in1=partner,
+                    op=ALU.add,
                 )
-                nc.vector.tensor_tensor(out=pair[:], in0=pair[:], in1=there[:, :, 0], op=ALU.mult)
+                nc.vector.tensor_tensor(
+                    out=pair[:], in0=pair[:], in1=slots[:, :, e : e + CS, RN_COL], op=ALU.mult
+                )
                 nc.vector.scalar_tensor_tensor(
                     out=alpha[:, ti, :],
-                    in0=pair[:],
+                    in0=pair[:].rearrange("p r cc -> p (r cc)"),
                     scalar=rn[:, ti : ti + 1],
-                    in1=in_row[:, e, :],
+                    in1=in_row[:, e].rearrange("p r cc -> p (r cc)"),
                     op0=ALU.mult,
                     op1=ALU.mult,
                 )
@@ -333,7 +353,7 @@ def tile_spatialcontext_t_v_kernel(tc, feature, conv_w, conv_b, z, grad_out, out
             bank = word_window(psum_s, g, dy, 0, half)
             for ep in range(2):
                 for e in range(2):
-                    k = (ep - e + PAD) * CS + dy + PAD
+                    k = (dy + PAD) * CS + ep - e + PAD
                     coeff = alpha[:, 2 * g + e, k : k + 1]
                     if dy == -PAD and ep == 0:
                         nc.scalar.activation(
@@ -369,7 +389,7 @@ def tile_spatialcontext_t_v_kernel(tc, feature, conv_w, conv_b, z, grad_out, out
                     for e in range(2):
                         dx = 2 * wsh + ep - e
                         if abs(dx) <= PAD and (dx != 0 or dy != 0):
-                            terms[e].append((bank, ep, (dx + PAD) * CS + dy + PAD))
+                            terms[e].append((bank, ep, (dy + PAD) * CS + dx + PAD))
             for turn in zip(terms[0], terms[1]):
                 for e in range(2):
                     bank, ep, k = turn[e]

@@ -135,10 +135,8 @@ def tile_spatialcontext_t_v_kernel(tc, feature, conv_w, conv_b, z, grad_out, out
                     in_=feat[b, (NT - 1) * P : C, :],
                 )
             w_grouped = stage_w.tile([P, PASSES, INC, PACK], BF16, align_bytes=64)
-            for c in range(PASSES):
-                nc.vector.tensor_copy(
-                    out=w_grouped[:, c], in_=w_raw[:, c].rearrange("p j i -> p i j")
-                )
+            nc.vector.tensor_copy(out=w_grouped[:, 0], in_=w_raw[:, 0].rearrange("p j i -> p i j"))
+            nc.scalar.copy(out=w_grouped[:, 1], in_=w_raw[:, 1].rearrange("p j i -> p i j"))
             for c in range(PASSES):
                 nc.vector.quantize_mx(
                     out=w_codes[:, c, :].bitcast(E4M3X4),
@@ -247,8 +245,12 @@ def tile_spatialcontext_t_v_kernel(tc, feature, conv_w, conv_b, z, grad_out, out
 
         def norm_floor(g):
             two = slice(2 * g, 2 * g + 2)
-            nc.vector.tensor_reduce(out=sq[:, two], in_=sq_half[:, two, :], axis=AX.X, op=ALU.add)
-            nc.vector.tensor_scalar_max(out=sq_floor[:, two], in0=sq[:, two], scalar1=EPS * EPS)
+            nc.gpsimd.tensor_tensor(
+                out=sq[:, two], in0=sq_half[:, two, 0], in1=sq_half[:, two, 1], op=ALU.add
+            )
+            nc.gpsimd.tensor_scalar(
+                out=sq_floor[:, two], in0=sq[:, two], scalar1=EPS * EPS, scalar2=0.0, op0=ALU.max, op1=ALU.add
+            )
 
         def norm_root(g):
             two = slice(2 * g, 2 * g + 2)
@@ -257,13 +259,20 @@ def tile_spatialcontext_t_v_kernel(tc, feature, conv_w, conv_b, z, grad_out, out
         def norm_inverse(g):
             two = slice(2 * g, 2 * g + 2)
             nc.vector.reciprocal(out=rn[:, two], in_=norm[:, two])
-            nc.vector.tensor_copy(out=own[:, two, RN_COL], in_=rn[:, two])
-            nc.vector.tensor_tensor(out=rn2[:, two], in0=rn[:, two], in1=rn[:, two], op=ALU.mult)
-            nc.vector.tensor_scalar_mul(out=neg_rn2[:, two], in0=rn2[:, two], scalar1=-1.0)
-            nc.vector.tensor_tensor(
+
+        def norm_powers(g):
+            two = slice(2 * g, 2 * g + 2)
+            nc.gpsimd.tensor_copy(out=own[:, two, RN_COL], in_=rn[:, two])
+            nc.gpsimd.tensor_tensor(out=rn2[:, two], in0=rn[:, two], in1=rn[:, two], op=ALU.mult)
+            nc.gpsimd.tensor_scalar(
+                out=neg_rn2[:, two], in0=rn2[:, two], scalar1=-1.0, scalar2=0.0, op0=ALU.mult, op1=ALU.add
+            )
+            nc.gpsimd.tensor_tensor(
                 out=off_unit[:, two], in0=neg_rn2[:, two], in1=sq[:, two], op=ALU.mult
             )
-            nc.vector.tensor_scalar_add(out=off_unit[:, two], in0=off_unit[:, two], scalar1=1.0)
+            nc.gpsimd.tensor_scalar(
+                out=off_unit[:, two], in0=off_unit[:, two], scalar1=1.0, scalar2=1.0, op0=ALU.mult, op1=ALU.add
+            )
 
         def store_own(g):
             b, d = divmod(g, GROUPS)
@@ -276,19 +285,21 @@ def tile_spatialcontext_t_v_kernel(tc, feature, conv_w, conv_b, z, grad_out, out
         def prepare_step(g, s):
             if s == 0:
                 mask_gradient(g)
+                own_features(g, 0)
             elif s == 1:
                 quantise_gradient(g)
+                own_features(g, 1)
             elif s < 4:
-                own_features(g, s - 2)
-            elif s < 6:
-                own_dx(g, s - 4)
-            elif s == 6:
+                own_dx(g, s - 2)
+            elif s == 4:
                 norm_floor(g)
-            elif s == 7:
+            elif s == 5:
                 norm_root(g)
-            elif s == 8:
+            elif s == 6:
                 norm_inverse(g)
-            else:
+            elif s == 7:
+                norm_powers(g)
+            elif s == 8:
                 store_own(g)
 
         def coeff_step(g, e, r):
@@ -314,24 +325,25 @@ def tile_spatialcontext_t_v_kernel(tc, feature, conv_w, conv_b, z, grad_out, out
                     "p (r x) -> p r x", x=row_step
                 )[:, :, 0 : (CS - 1) * col_step + 1 : col_step]
                 pair = small.tile([P, CS, CS], F32, name="pair")
-                nc.vector.tensor_tensor(
+                nc.gpsimd.tensor_tensor(
                     out=pair[:],
                     in0=own[:, ti, DV0:OWN_W].rearrange("p (cc r) -> p r cc", r=CS),
                     in1=partner,
                     op=ALU.add,
                 )
-                nc.vector.tensor_tensor(
+                nc.gpsimd.tensor_tensor(
                     out=pair[:], in0=pair[:], in1=slots[:, :, e : e + CS, RN_COL], op=ALU.mult
                 )
-                nc.vector.scalar_tensor_tensor(
+                nc.gpsimd.tensor_tensor(out=pair[:], in0=pair[:], in1=in_row[:, e], op=ALU.mult)
+                nc.gpsimd.tensor_scalar(
                     out=alpha[:, ti, :],
                     in0=pair[:].rearrange("p r cc -> p (r cc)"),
-                    scalar=rn[:, ti : ti + 1],
-                    in1=in_row[:, e].rearrange("p r cc -> p (r cc)"),
+                    scalar1=rn[:, ti : ti + 1],
+                    scalar2=0.0,
                     op0=ALU.mult,
-                    op1=ALU.mult,
+                    op1=ALU.add,
                 )
-                nc.vector.tensor_tensor(
+                nc.gpsimd.tensor_tensor(
                     out=centre[:, ti : ti + 1],
                     in0=alpha[:, ti, CENTRE : CENTRE + 1],
                     in1=off_unit[:, ti : ti + 1],
@@ -339,7 +351,7 @@ def tile_spatialcontext_t_v_kernel(tc, feature, conv_w, conv_b, z, grad_out, out
                 )
 
         def middle_on_pool(g, dy):
-            return dy == -PAD or (g > 0 and dy != 0)
+            return dy == -PAD or g > 0
 
         def pool_step(g, half, dy):
             if half == 0 and dy == -PAD:
@@ -354,6 +366,8 @@ def tile_spatialcontext_t_v_kernel(tc, feature, conv_w, conv_b, z, grad_out, out
             for ep in range(2):
                 for e in range(2):
                     k = (dy + PAD) * CS + ep - e + PAD
+                    if k == CENTRE:
+                        continue
                     coeff = alpha[:, 2 * g + e, k : k + 1]
                     if dy == -PAD and ep == 0:
                         nc.scalar.activation(

@@ -36,9 +36,11 @@ F_PAD = 128
 OWN_W = 32
 DV0 = OWN_W - NK
 RN_COL = DV0 - 1
+SLOTS = 6
 MARGIN = 128
 SCR_CH = (HW + 2 * MARGIN) * OWN_W // HW
 THERE_W = 1024
+STEPS = 2 * CS
 EARLY = 2
 
 FLOPS = 2 * OC * INC * B * HW + 4 * NK * C * B * HW
@@ -50,6 +52,10 @@ def tile_spatialcontext_t_v_kernel(tc, feature, conv_w, conv_b, z, grad_out, out
     z_in = z.rearrange("b o h w -> b o (h w)")
     g_in = grad_out.rearrange("b o h w -> b o (h w)")
     res = out.rearrange("b c h w -> b c (h w)")
+    scratch = [
+        out[B - 1, C - (B - b) * SCR_CH : C - (B - b - 1) * SCR_CH].rearrange("c h w -> (c h) w")
+        for b in range(B)
+    ]
 
     with ExitStack() as ctx:
         keep = ctx.enter_context(tc.tile_pool(name="keep", bufs=1))
@@ -82,6 +88,8 @@ def tile_spatialcontext_t_v_kernel(tc, feature, conv_w, conv_b, z, grad_out, out
                         out=in_row[:, e, :, cc],
                         in_=inside[:, side : side + 1].to_broadcast([P, CS]),
                     )
+        zeros = keep.tile([P, OWN_W], F32)
+        nc.vector.memset(zeros[:], 0.0)
 
         f_sb = keep.tile([P, 2 * F_PAD + B * NT * HW], BF16)
         f_words = f_sb[:].bitcast(F32)
@@ -95,17 +103,8 @@ def tile_spatialcontext_t_v_kernel(tc, feature, conv_w, conv_b, z, grad_out, out
         w_scales = keep.tile([P, PASSES, INC], U8, align_bytes=64)
         dz_codes = keep.tile([P, NG, PASSES, 2 * P], U32, align_bytes=64)
         dz_scales = keep.tile([P, NG, PASSES, 2 * P], U8, align_bytes=64)
-        own = keep.tile([P, 2 * NG, OWN_W], F32)
-        scratch = [
-            out[B - 1, C - (B - b) * SCR_CH : C - (B - b - 1) * SCR_CH].rearrange("c h w -> (c h) w")
-            for b in range(B)
-        ]
-        zeros = keep.tile([P, OWN_W], F32)
-        nc.vector.memset(zeros[:], 0.0)
-        for b in range(B):
-            nc.sync.dma_start(out=scratch[b][0:MARGIN, :], in_=zeros[:])
-            nc.sync.dma_start(out=scratch[b][MARGIN + HW : 2 * MARGIN + HW, :], in_=zeros[:])
         f_own = keep.tile([P, NG, 2 * INC], BF16)
+        own = keep.tile([P, 2 * NG, OWN_W], F32)
         alpha = keep.tile([P, 2 * NG, NK], F32)
         sq_half = keep.tile([P, 2 * NG, 2], F32)
         sq = keep.tile([P, 2 * NG], F32)
@@ -113,27 +112,28 @@ def tile_spatialcontext_t_v_kernel(tc, feature, conv_w, conv_b, z, grad_out, out
         norm = keep.tile([P, 2 * NG], F32)
         rn = keep.tile([P, 2 * NG], F32)
         rn2 = keep.tile([P, 2 * NG], F32)
-        neg_rn2 = keep.tile([P, 2 * NG], F32)
         off_unit = keep.tile([P, 2 * NG], F32)
         centre = keep.tile([P, 2 * NG], F32)
 
         stage_z = ctx.enter_context(tc.tile_pool(name="stage_z", bufs=2))
+
+        def load_features(b):
+            base = F_PAD + b * NT * HW
+            nc.sync.dma_start(
+                out=f_sb[:, base : base + (NT - 1) * HW].rearrange("p (t x) -> p t x", x=HW),
+                in_=feat[b, 0 : (NT - 1) * P, :].rearrange("(t p) x -> p t x", p=P),
+            )
+            nc.sync.dma_start(
+                out=f_sb[0:C_TAIL, base + (NT - 1) * HW : base + NT * HW],
+                in_=feat[b, (NT - 1) * P : C, :],
+            )
 
         with tc.tile_pool(name="stage_w", bufs=1) as stage_w:
             w_raw = stage_w.tile([P, PASSES, PACK, INC], BF16)
             nc.sync.dma_start(
                 out=w_raw[:], in_=conv_w.rearrange("(c p j) i -> p c j i", p=P, j=PACK)
             )
-            for b in range(B):
-                base = F_PAD + b * NT * HW
-                nc.sync.dma_start(
-                    out=f_sb[:, base : base + (NT - 1) * HW].rearrange("p (t x) -> p t x", x=HW),
-                    in_=feat[b, 0 : (NT - 1) * P, :].rearrange("(t p) x -> p t x", p=P),
-                )
-                nc.sync.dma_start(
-                    out=f_sb[0:C_TAIL, base + (NT - 1) * HW : base + NT * HW],
-                    in_=feat[b, (NT - 1) * P : C, :],
-                )
+            load_features(0)
             w_grouped = stage_w.tile([P, PASSES, INC, PACK], BF16, align_bytes=64)
             nc.vector.tensor_copy(out=w_grouped[:, 0], in_=w_raw[:, 0].rearrange("p j i -> p i j"))
             nc.scalar.copy(out=w_grouped[:, 1], in_=w_raw[:, 1].rearrange("p j i -> p i j"))
@@ -147,7 +147,7 @@ def tile_spatialcontext_t_v_kernel(tc, feature, conv_w, conv_b, z, grad_out, out
         small = ctx.enter_context(tc.tile_pool(name="small", bufs=3))
         scrap_pool = ctx.enter_context(tc.tile_pool(name="scrap", bufs=2))
         acc_pool = ctx.enter_context(tc.tile_pool(name="acc", bufs=3))
-        prod_pool = ctx.enter_context(tc.tile_pool(name="prod", bufs=4))
+        prod_pool = ctx.enter_context(tc.tile_pool(name="prod", bufs=6))
         fin_pool = ctx.enter_context(tc.tile_pool(name="fin", bufs=2))
         fetch_pool = ctx.enter_context(tc.tile_pool(name="fetch", bufs=2))
         accs = {}
@@ -165,8 +165,8 @@ def tile_spatialcontext_t_v_kernel(tc, feature, conv_w, conv_b, z, grad_out, out
                 )
             return bank
 
-        def pixel_of_words(words, ep, width):
-            return words.bitcast(BF16).rearrange("p (c e) -> p c e", e=2)[:, 0:width, ep]
+        def pixel_of_words(pairs, ep, width):
+            return pairs.rearrange("p (c e) -> p c e", e=2)[:, 0:width, ep]
 
         def dx_group(g, e, half, bank):
             cols = slice(e * P, (e + 1) * P)
@@ -217,23 +217,21 @@ def tile_spatialcontext_t_v_kernel(tc, feature, conv_w, conv_b, z, grad_out, out
             live[("dz", g)] = dz_t
 
         def quantise_gradient(g):
-            for c in range(PASSES):
-                nc.vector.quantize_mx(
-                    out=dz_codes[:, g, c, :].bitcast(E5M2X4),
-                    scales=dz_scales[:, g, c, :],
-                    in_=live[("dz", g)][:, c].rearrange("p e m j -> p (e m j)"),
-                )
+            nc.vector.quantize_mx(
+                out=dz_codes[:, g].rearrange("p c x -> p (c x)").bitcast(E5M2X4),
+                scales=dz_scales[:, g].rearrange("p c x -> p (c x)"),
+                in_=live[("dz", g)][:].rearrange("p c e m j -> p (c e m j)"),
+            )
 
         def own_features(g, half):
             bank = word_window(psum_s, g, 0, 0, half)
-            nc.scalar.copy(
-                out=f_own[:, g, half * 2 * HALF : (half + 1) * 2 * HALF], in_=bank[:].bitcast(BF16)
-            )
+            pairs = bank[:].bitcast(BF16)
+            nc.scalar.copy(out=f_own[:, g, half * 2 * HALF : (half + 1) * 2 * HALF], in_=pairs)
             for e in range(2):
                 squares = scrap_pool.tile([P, HALF], F32, name="squares")
                 nc.scalar.activation(
                     out=squares[:],
-                    in_=pixel_of_words(bank[:], e, HALF),
+                    in_=pixel_of_words(pairs, e, HALF),
                     func=ACT.Square,
                     accum_out=sq_half[:, 2 * g + e, half : half + 1],
                 )
@@ -249,7 +247,12 @@ def tile_spatialcontext_t_v_kernel(tc, feature, conv_w, conv_b, z, grad_out, out
                 out=sq[:, two], in0=sq_half[:, two, 0], in1=sq_half[:, two, 1], op=ALU.add
             )
             nc.gpsimd.tensor_scalar(
-                out=sq_floor[:, two], in0=sq[:, two], scalar1=EPS * EPS, scalar2=0.0, op0=ALU.max, op1=ALU.add
+                out=sq_floor[:, two],
+                in0=sq[:, two],
+                scalar1=EPS * EPS,
+                scalar2=0.0,
+                op0=ALU.max,
+                op1=ALU.add,
             )
 
         def norm_root(g):
@@ -264,14 +267,14 @@ def tile_spatialcontext_t_v_kernel(tc, feature, conv_w, conv_b, z, grad_out, out
             two = slice(2 * g, 2 * g + 2)
             nc.gpsimd.tensor_copy(out=own[:, two, RN_COL], in_=rn[:, two])
             nc.gpsimd.tensor_tensor(out=rn2[:, two], in0=rn[:, two], in1=rn[:, two], op=ALU.mult)
+            nc.gpsimd.tensor_tensor(out=off_unit[:, two], in0=rn2[:, two], in1=sq[:, two], op=ALU.mult)
             nc.gpsimd.tensor_scalar(
-                out=neg_rn2[:, two], in0=rn2[:, two], scalar1=-1.0, scalar2=0.0, op0=ALU.mult, op1=ALU.add
-            )
-            nc.gpsimd.tensor_tensor(
-                out=off_unit[:, two], in0=neg_rn2[:, two], in1=sq[:, two], op=ALU.mult
-            )
-            nc.gpsimd.tensor_scalar(
-                out=off_unit[:, two], in0=off_unit[:, two], scalar1=1.0, scalar2=1.0, op0=ALU.mult, op1=ALU.add
+                out=off_unit[:, two],
+                in0=off_unit[:, two],
+                scalar1=-1.0,
+                scalar2=1.0,
+                op0=ALU.mult,
+                op1=ALU.add,
             )
 
         def store_own(g):
@@ -307,7 +310,9 @@ def tile_spatialcontext_t_v_kernel(tc, feature, conv_w, conv_b, z, grad_out, out
             ti = 2 * g + e
             if e == 0 and r == 0:
                 there = fetch_pool.tile([P, THERE_W], F32, name="there")
-                slots = there[:, 0 : CS * 6 * OWN_W].rearrange("p (r j w) -> p r j w", r=CS, j=6)
+                slots = there[:, 0 : CS * SLOTS * OWN_W].rearrange(
+                    "p (r j w) -> p r j w", r=CS, j=SLOTS
+                )
                 for rr in range(CS):
                     for wsh in (-1, 0, 1):
                         first = MARGIN + 2 * P * d + 2 * wsh + 2 * ROW_WORDS * (rr - PAD)
@@ -318,9 +323,11 @@ def tile_spatialcontext_t_v_kernel(tc, feature, conv_w, conv_b, z, grad_out, out
                 live["there"] = there
             if r == CS - 1:
                 there = live["there"]
-                slots = there[:, 0 : CS * 6 * OWN_W].rearrange("p (r j w) -> p r j w", r=CS, j=6)
+                slots = there[:, 0 : CS * SLOTS * OWN_W].rearrange(
+                    "p (r j w) -> p r j w", r=CS, j=SLOTS
+                )
                 start = e * OWN_W + OWN_W - 1
-                row_step, col_step = 6 * OWN_W - 1, OWN_W - CS
+                row_step, col_step = SLOTS * OWN_W - 1, OWN_W - CS
                 partner = there[:, start : start + CS * row_step].rearrange(
                     "p (r x) -> p r x", x=row_step
                 )[:, :, 0 : (CS - 1) * col_step + 1 : col_step]
@@ -351,7 +358,7 @@ def tile_spatialcontext_t_v_kernel(tc, feature, conv_w, conv_b, z, grad_out, out
                 )
 
         def middle_on_pool(g, dy):
-            return dy == -PAD or g > 0
+            return dy == -PAD or (g > 0 and dy != 0)
 
         def pool_step(g, half, dy):
             if half == 0 and dy == -PAD:
@@ -362,27 +369,25 @@ def tile_spatialcontext_t_v_kernel(tc, feature, conv_w, conv_b, z, grad_out, out
                 return
             acc = accs[g]
             width = width_of(half)
-            bank = word_window(psum_s, g, dy, 0, half)
+            pairs = word_window(psum_s, g, dy, 0, half)[:].bitcast(BF16)
             for ep in range(2):
                 for e in range(2):
                     k = (dy + PAD) * CS + ep - e + PAD
-                    if k == CENTRE:
-                        continue
-                    coeff = alpha[:, 2 * g + e, k : k + 1]
+                    factor = alpha[:, 2 * g + e, k : k + 1]
                     if dy == -PAD and ep == 0:
                         nc.scalar.activation(
                             out=acc[e][:, half * HALF : (half + 1) * HALF],
-                            in_=pixel_of_words(bank[:], ep, HALF),
+                            in_=pixel_of_words(pairs, ep, HALF),
                             func=ACT.Copy,
-                            scale=coeff,
+                            scale=factor,
                         )
                     else:
                         prod = prod_pool.tile([P, HALF], F32, name="prod")
                         nc.scalar.activation(
                             out=prod[:, 0:width],
-                            in_=pixel_of_words(bank[:], ep, width),
+                            in_=pixel_of_words(pairs, ep, width),
                             func=ACT.Copy,
-                            scale=coeff,
+                            scale=factor,
                         )
                         nc.gpsimd.tensor_tensor(
                             out=acc[e][:, half * HALF : half * HALF + width],
@@ -398,53 +403,41 @@ def tile_spatialcontext_t_v_kernel(tc, feature, conv_w, conv_b, z, grad_out, out
             for wsh in (-1, 0, 1):
                 if wsh == 0 and middle_on_pool(g, dy):
                     continue
-                bank = word_window(psum_v, g, dy, wsh, half)
+                pairs = word_window(psum_v, g, dy, wsh, half)[:].bitcast(BF16)
                 for ep in range(2):
                     for e in range(2):
                         dx = 2 * wsh + ep - e
                         if abs(dx) <= PAD and (dx != 0 or dy != 0):
-                            terms[e].append((bank, ep, (dy + PAD) * CS + dx + PAD))
+                            terms[e].append((pairs, ep, (dy + PAD) * CS + dx + PAD))
             for turn in zip(terms[0], terms[1]):
                 for e in range(2):
-                    bank, ep, k = turn[e]
+                    pairs, ep, k = turn[e]
                     nc.vector.scalar_tensor_tensor(
                         out=acc[e][:, half * HALF : half * HALF + width],
-                        in0=pixel_of_words(bank[:], ep, width),
+                        in0=pixel_of_words(pairs, ep, width),
                         scalar=alpha[:, 2 * g + e, k : k + 1],
                         in1=acc[e][:, half * HALF : half * HALF + width],
                         op0=ALU.mult,
                         op1=ALU.add,
                     )
 
-        def own_feature(g, half, e, width):
-            words = f_own[:, g, half * 2 * HALF : (half + 1) * 2 * HALF].bitcast(F32)
-            return pixel_of_words(words, e, width)
-
         def project(g):
-            acc = accs[g]
-            dots = small.tile([P, 2, 2], F32, name="dots")
-            for e in range(2):
-                for half in range(2):
-                    width = width_of(half)
-                    scrap = scrap_pool.tile([P, HALF], F32, name="scrap")
-                    nc.vector.scalar_tensor_tensor(
-                        out=scrap[:, 0:width],
-                        in0=own_feature(g, half, e, width),
-                        scalar=1.0,
-                        in1=acc[e][:, half * HALF : half * HALF + width],
-                        op0=ALU.mult,
-                        op1=ALU.mult,
-                        accum_out=dots[:, e, half : half + 1],
-                    )
+            two = slice(2 * g, 2 * g + 2)
             dot = small.tile([P, 2], F32, name="dot")
-            nc.vector.tensor_reduce(out=dot[:], in_=dots[:], axis=AX.X, op=ALU.add)
+            for e in range(2):
+                scrap = scrap_pool.tile([P, C], F32, name="scrap")
+                nc.vector.scalar_tensor_tensor(
+                    out=scrap[:],
+                    in0=pixel_of_words(f_own[:, g, :], e, C),
+                    scalar=1.0,
+                    in1=accs[g][e][:, 0:C],
+                    op0=ALU.mult,
+                    op1=ALU.mult,
+                    accum_out=dot[:, e : e + 1],
+                )
             gamma = small.tile([P, 2], F32, name="gamma")
-            nc.vector.tensor_tensor(
-                out=gamma[:], in0=dot[:], in1=neg_rn2[:, 2 * g : 2 * g + 2], op=ALU.mult
-            )
-            nc.vector.tensor_tensor(
-                out=gamma[:], in0=gamma[:], in1=centre[:, 2 * g : 2 * g + 2], op=ALU.add
-            )
+            nc.vector.tensor_tensor(out=gamma[:], in0=dot[:], in1=rn2[:, two], op=ALU.mult)
+            nc.vector.tensor_tensor(out=gamma[:], in0=centre[:, two], in1=gamma[:], op=ALU.subtract)
             gammas[g] = gamma
 
         def finish_step(g, half, j):
@@ -455,7 +448,7 @@ def tile_spatialcontext_t_v_kernel(tc, feature, conv_w, conv_b, z, grad_out, out
                 along = fin_pool.tile([P, HALF], F32, tag="along%d" % e, name="along%d" % e)
                 nc.scalar.activation(
                     out=along[:],
-                    in_=own_feature(g, half, e, HALF),
+                    in_=pixel_of_words(f_own[:, g, 2 * lo : 2 * (lo + HALF)], e, HALF),
                     func=ACT.Copy,
                     scale=gammas[g][:, e : e + 1],
                 )
@@ -501,7 +494,11 @@ def tile_spatialcontext_t_v_kernel(tc, feature, conv_w, conv_b, z, grad_out, out
         with tc.manual_schedule():
             for g in range(EARLY):
                 load_gradient(g)
-            for s in range(2 * CS):
+            for b in range(B):
+                nc.sync.dma_start(out=scratch[b][0:MARGIN, :], in_=zeros[:])
+                nc.sync.dma_start(out=scratch[b][MARGIN + HW : 2 * MARGIN + HW, :], in_=zeros[:])
+            load_features(1)
+            for s in range(STEPS):
                 for g in range(EARLY):
                     prepare_step(g, s)
             load_gradient(EARLY)

from contextlib import ExitStack

import concourse.mybir as mybir
from concourse.masks import make_identity

F32 = mybir.dt.float32
BF16 = mybir.dt.bfloat16
U32 = mybir.dt.uint32
U8 = mybir.dt.uint8
E4M3X4 = mybir.dt.float8_e4m3fn_x4
E5M2X4 = mybir.dt.float8_e5m2_x4
ALU = mybir.AluOpType
ACT = mybir.ActivationFunctionType
AX = mybir.AxisListType

P = 128
B, C, OC, HW = 2, 999, 1024, 1024
CS = 5
PAD = CS // 2
NK = CS * CS
CENTRE = NK // 2
INC = C + NK
EPS = 1e-12
PACK = 4
K_PASS = P * PACK
PASSES = OC // K_PASS
NT = INC // P
C_TAIL = C - (NT - 1) * P
ZERO_FROM = 96
WORDS = HW // 2
ROW_WORDS = 16
GROUPS = WORDS // P
NG = B * GROUPS
HALF = 512
F_PAD = 128
OWN_W = 32
DV0 = OWN_W - NK
RN_COL = DV0 - 1
SLOTS = 6
MARGIN = 128
SCR_CH = (HW + 2 * MARGIN) * OWN_W // HW
THERE_W = 1024
STEPS = 2 * CS
EARLY = 2

FLOPS = 2 * OC * INC * B * HW + 4 * NK * C * B * HW


def tile_spatialcontext_t_v_kernel(tc, feature, conv_w, conv_b, z, grad_out, out):
    nc = tc.nc
    feat = feature.rearrange("b c h w -> b c (h w)")
    z_in = z.rearrange("b o h w -> b o (h w)")
    g_in = grad_out.rearrange("b o h w -> b o (h w)")
    res = out.rearrange("b c h w -> b c (h w)")
    scratch = [
        out[B - 1, C - (B - b) * SCR_CH : C - (B - b - 1) * SCR_CH].rearrange("c h w -> (c h) w")
        for b in range(B)
    ]

    with ExitStack() as ctx:
        keep = ctx.enter_context(tc.tile_pool(name="keep", bufs=1))
        psum_v = ctx.enter_context(tc.psum_pool(name="psum_v", bufs=4))
        psum_s = ctx.enter_context(tc.psum_pool(name="psum_s", bufs=2))
        psum_mx = ctx.enter_context(tc.psum_pool(name="psum_mx", bufs=1))
        psum_o = ctx.enter_context(tc.psum_pool(name="psum_o", bufs=1))

        ident = keep.tile([P, P], F32)
        make_identity(nc, ident[:])

        ident_rows = ident[:].rearrange("p (r u) -> p r u", u=ROW_WORDS)
        at_edge = keep.tile([P, 2], F32)
        nc.vector.tensor_reduce(out=at_edge[:, 0:1], in_=ident_rows[:, :, 0], axis=AX.X, op=ALU.add)
        nc.vector.tensor_reduce(
            out=at_edge[:, 1:2], in_=ident_rows[:, :, ROW_WORDS - 1], axis=AX.X, op=ALU.add
        )
        inside = keep.tile([P, 2], F32)
        nc.vector.tensor_scalar(
            out=inside[:], in0=at_edge[:], scalar1=-1.0, scalar2=1.0, op0=ALU.mult, op1=ALU.add
        )
        in_row = keep.tile([P, 2, CS, CS], F32)
        nc.vector.memset(in_row[:], 1.0)
        for e in range(2):
            for cc in range(CS):
                wsh = (e + cc - PAD) // 2
                if wsh != 0:
                    side = 0 if wsh < 0 else 1
                    nc.vector.tensor_copy(
                        out=in_row[:, e, :, cc],
                        in_=inside[:, side : side + 1].to_broadcast([P, CS]),
                    )
        zeros = keep.tile([P, OWN_W], F32)
        nc.vector.memset(zeros[:], 0.0)

        f_sb = keep.tile([P, 2 * F_PAD + B * NT * HW], BF16)
        f_words = f_sb[:].bitcast(F32)
        nc.vector.memset(f_sb[:, 0:F_PAD], 0.0)
        nc.vector.memset(f_sb[:, F_PAD + B * NT * HW :], 0.0)
        for b in range(B):
            last = F_PAD + (b * NT + NT - 1) * HW
            nc.vector.memset(f_sb[ZERO_FROM:P, last : last + HW], 0.0)

        w_codes = keep.tile([P, PASSES, INC], U32, align_bytes=64)
        w_scales = keep.tile([P, PASSES, INC], U8, align_bytes=64)
        dz_codes = keep.tile([P, NG, PASSES, 2 * P], U32, align_bytes=64)
        dz_scales = keep.tile([P, NG, PASSES, 2 * P], U8, align_bytes=64)
        f_own = keep.tile([P, NG, 2 * INC], BF16)
        own = keep.tile([P, 2 * NG, OWN_W], F32)
        alpha = keep.tile([P, 2 * NG, NK], F32)
        sq_half = keep.tile([P, 2 * NG, 2], F32)
        sq = keep.tile([P, 2 * NG], F32)
        sq_floor = keep.tile([P, 2 * NG], F32)
        norm = keep.tile([P, 2 * NG], F32)
        rn = keep.tile([P, 2 * NG], F32)
        rn2 = keep.tile([P, 2 * NG], F32)
        off_unit = keep.tile([P, 2 * NG], F32)
        centre = keep.tile([P, 2 * NG], F32)

        stage_z = ctx.enter_context(tc.tile_pool(name="stage_z", bufs=2))

        def load_features(b):
            base = F_PAD + b * NT * HW
            nc.sync.dma_start(
                out=f_sb[:, base : base + (NT - 1) * HW].rearrange("p (t x) -> p t x", x=HW),
                in_=feat[b, 0 : (NT - 1) * P, :].rearrange("(t p) x -> p t x", p=P),
            )
            nc.sync.dma_start(
                out=f_sb[0:C_TAIL, base + (NT - 1) * HW : base + NT * HW],
                in_=feat[b, (NT - 1) * P : C, :],
            )

        with tc.tile_pool(name="stage_w", bufs=1) as stage_w:
            w_raw = stage_w.tile([P, PASSES, PACK, INC], BF16)
            nc.sync.dma_start(
                out=w_raw[:], in_=conv_w.rearrange("(c p j) i -> p c j i", p=P, j=PACK)
            )
            load_features(0)
            w_grouped = stage_w.tile([P, PASSES, INC, PACK], BF16, align_bytes=64)
            nc.vector.tensor_copy(out=w_grouped[:, 0], in_=w_raw[:, 0].rearrange("p j i -> p i j"))
            nc.scalar.copy(out=w_grouped[:, 1], in_=w_raw[:, 1].rearrange("p j i -> p i j"))
            for c in range(PASSES):
                nc.vector.quantize_mx(
                    out=w_codes[:, c, :].bitcast(E4M3X4),
                    scales=w_scales[:, c, :],
                    in_=w_grouped[:, c].rearrange("p i j -> p (i j)"),
                )

        small = ctx.enter_context(tc.tile_pool(name="small", bufs=3))
        scrap_pool = ctx.enter_context(tc.tile_pool(name="scrap", bufs=2))
        acc_pool = ctx.enter_context(tc.tile_pool(name="acc", bufs=3))
        prod_pool = ctx.enter_context(tc.tile_pool(name="prod", bufs=6))
        fin_pool = ctx.enter_context(tc.tile_pool(name="fin", bufs=2))
        fetch_pool = ctx.enter_context(tc.tile_pool(name="fetch", bufs=2))
        accs = {}
        gammas = {}
        live = {}

        def word_window(pool, g, dy, wsh, half):
            b, d = divmod(g, GROUPS)
            bank = pool.tile([P, HALF], F32, tag="window", name="window")
            for u in range(HALF // P):
                t = half * (HALF // P) + u
                w0 = F_PAD // 2 + (b * NT + t) * WORDS + P * d + wsh + ROW_WORDS * dy
                nc.tensor.transpose(
                    out=bank[:, u * P : (u + 1) * P], in_=f_words[:, w0 : w0 + P], identity=ident[:]
                )
            return bank

        def pixel_of_words(pairs, ep, width):
            return pairs.rearrange("p (c e) -> p c e", e=2)[:, 0:width, ep]

        def dx_group(g, e, half, bank):
            cols = slice(e * P, (e + 1) * P)
            for c in range(PASSES):
                nc.tensor.matmul_mx(
                    out=bank[:],
                    lhsT=dz_codes[:, g, c, cols].bitcast(E5M2X4),
                    lhsT_scale=dz_scales[:, g, c, cols],
                    rhs=w_codes[:, c, half * HALF : (half + 1) * HALF].bitcast(E4M3X4),
                    rhs_scale=w_scales[:, c, half * HALF : (half + 1) * HALF],
                    start=(c == 0),
                    stop=(c == PASSES - 1),
                )

        def width_of(half):
            return HALF if half == 0 else C - HALF

        def load_gradient(g):
            b, d = divmod(g, GROUPS)
            px = slice(2 * P * d, 2 * P * (d + 1))
            z_t = stage_z.tile([P, PASSES, PACK, 2 * P], F32, name="z_t")
            g_t = stage_z.tile([P, PASSES, PACK, 2 * P], BF16, name="g_t")
            for c in range(PASSES):
                o_rows = slice(c * K_PASS, (c + 1) * K_PASS)
                nc.sync.dma_start(
                    out=z_t[:, c], in_=z_in[b, o_rows, px].rearrange("(p j) x -> p j x", j=PACK)
                )
                nc.sync.dma_start(
                    out=g_t[:, c], in_=g_in[b, o_rows, px].rearrange("(p j) x -> p j x", j=PACK)
                )
            live[("z", g)] = z_t
            live[("g", g)] = g_t

        def mask_gradient(g):
            dz_t = stage_z.tile([P, PASSES, 2, P, PACK], BF16, name="dz_t", align_bytes=64)
            for c in range(PASSES):
                z_par = live[("z", g)][:, c].rearrange("p j (m e) -> p e m j", e=2)
                g_par = live[("g", g)][:, c].rearrange("p j (m e) -> p e m j", e=2)
                for e in range(2):
                    nc.vector.scalar_tensor_tensor(
                        out=dz_t[:, c, e],
                        in0=z_par[:, e],
                        scalar=0.0,
                        in1=g_par[:, e],
                        op0=ALU.is_gt,
                        op1=ALU.mult,
                    )
            live[("dz", g)] = dz_t

        def quantise_gradient(g):
            nc.vector.quantize_mx(
                out=dz_codes[:, g].rearrange("p c x -> p (c x)").bitcast(E5M2X4),
                scales=dz_scales[:, g].rearrange("p c x -> p (c x)"),
                in_=live[("dz", g)][:].rearrange("p c e m j -> p (c e m j)"),
            )

        def own_features(g, half):
            bank = word_window(psum_s, g, 0, 0, half)
            pairs = bank[:].bitcast(BF16)
            nc.scalar.copy(out=f_own[:, g, half * 2 * HALF : (half + 1) * 2 * HALF], in_=pairs)
            for e in range(2):
                squares = scrap_pool.tile([P, HALF], F32, name="squares")
                nc.scalar.activation(
                    out=squares[:],
                    in_=pixel_of_words(pairs, e, HALF),
                    func=ACT.Square,
                    accum_out=sq_half[:, 2 * g + e, half : half + 1],
                )

        def own_dx(g, e):
            bank = psum_mx.tile([P, HALF], F32, tag="dx", name="dx")
            dx_group(g, e, 1, bank)
            nc.scalar.copy(out=own[:, 2 * g + e, :], in_=bank[:, HALF - OWN_W : HALF])

        def norm_floor(g):
            two = slice(2 * g, 2 * g + 2)
            nc.gpsimd.tensor_tensor(
                out=sq[:, two], in0=sq_half[:, two, 0], in1=sq_half[:, two, 1], op=ALU.add
            )
            nc.gpsimd.tensor_scalar(
                out=sq_floor[:, two],
                in0=sq[:, two],
                scalar1=EPS * EPS,
                scalar2=0.0,
                op0=ALU.max,
                op1=ALU.add,
            )

        def norm_root(g):
            two = slice(2 * g, 2 * g + 2)
            nc.scalar.activation(out=norm[:, two], in_=sq_floor[:, two], func=ACT.Sqrt)

        def norm_inverse(g):
            two = slice(2 * g, 2 * g + 2)
            nc.vector.reciprocal(out=rn[:, two], in_=norm[:, two])

        def norm_powers(g):
            two = slice(2 * g, 2 * g + 2)
            nc.gpsimd.tensor_copy(out=own[:, two, RN_COL], in_=rn[:, two])
            nc.gpsimd.tensor_tensor(out=rn2[:, two], in0=rn[:, two], in1=rn[:, two], op=ALU.mult)
            nc.gpsimd.tensor_tensor(out=off_unit[:, two], in0=rn2[:, two], in1=sq[:, two], op=ALU.mult)
            nc.gpsimd.tensor_scalar(
                out=off_unit[:, two],
                in0=off_unit[:, two],
                scalar1=-1.0,
                scalar2=1.0,
                op0=ALU.mult,
                op1=ALU.add,
            )

        def store_own(g):
            b, d = divmod(g, GROUPS)
            first = MARGIN + 2 * P * d
            nc.sync.dma_start(
                out=scratch[b][first : first + 2 * P, :].rearrange("(m e) w -> m e w", e=2),
                in_=own[:, 2 * g : 2 * g + 2, :],
            )

        def prepare_step(g, s):
            if s == 0:
                mask_gradient(g)
                own_features(g, 0)
            elif s == 1:
                quantise_gradient(g)
                own_features(g, 1)
            elif s < 4:
                own_dx(g, s - 2)
            elif s == 4:
                norm_floor(g)
            elif s == 5:
                norm_root(g)
            elif s == 6:
                norm_inverse(g)
            elif s == 7:
                norm_powers(g)
            elif s == 8:
                store_own(g)

        def coeff_step(g, e, r):
            b, d = divmod(g, GROUPS)
            ti = 2 * g + e
            if e == 0 and r == 0:
                there = fetch_pool.tile([P, THERE_W], F32, name="there")
                slots = there[:, 0 : CS * SLOTS * OWN_W].rearrange(
                    "p (r j w) -> p r j w", r=CS, j=SLOTS
                )
                for rr in range(CS):
                    for wsh in (-1, 0, 1):
                        first = MARGIN + 2 * P * d + 2 * wsh + 2 * ROW_WORDS * (rr - PAD)
                        nc.sync.dma_start(
                            out=slots[:, rr, 2 * (wsh + 1) : 2 * (wsh + 2), :],
                            in_=scratch[b][first : first + 2 * P, :].rearrange("(m e) w -> m e w", e=2),
                        )
                live["there"] = there
            if r == CS - 1:
                there = live["there"]
                slots = there[:, 0 : CS * SLOTS * OWN_W].rearrange(
                    "p (r j w) -> p r j w", r=CS, j=SLOTS
                )
                start = e * OWN_W + OWN_W - 1
                row_step, col_step = SLOTS * OWN_W - 1, OWN_W - CS
                partner = there[:, start : start + CS * row_step].rearrange(
                    "p (r x) -> p r x", x=row_step
                )[:, :, 0 : (CS - 1) * col_step + 1 : col_step]
                pair = small.tile([P, CS, CS], F32, name="pair")
                nc.gpsimd.tensor_tensor(
                    out=pair[:],
                    in0=own[:, ti, DV0:OWN_W].rearrange("p (cc r) -> p r cc", r=CS),
                    in1=partner,
                    op=ALU.add,
                )
                nc.gpsimd.tensor_tensor(
                    out=pair[:], in0=pair[:], in1=slots[:, :, e : e + CS, RN_COL], op=ALU.mult
                )
                nc.gpsimd.tensor_tensor(out=pair[:], in0=pair[:], in1=in_row[:, e], op=ALU.mult)
                nc.gpsimd.tensor_scalar(
                    out=alpha[:, ti, :],
                    in0=pair[:].rearrange("p r cc -> p (r cc)"),
                    scalar1=rn[:, ti : ti + 1],
                    scalar2=0.0,
                    op0=ALU.mult,
                    op1=ALU.add,
                )
                nc.gpsimd.tensor_tensor(
                    out=centre[:, ti : ti + 1],
                    in0=alpha[:, ti, CENTRE : CENTRE + 1],
                    in1=off_unit[:, ti : ti + 1],
                    op=ALU.mult,
                )

        def middle_on_pool(g, dy):
            return dy == -PAD or (g > 0 and dy != 0)

        def pool_step(g, half, dy):
            if half == 0 and dy == -PAD:
                accs[g] = [
                    acc_pool.tile([P, INC], F32, tag="acc%d" % e, name="acc%d" % e) for e in range(2)
                ]
            if not middle_on_pool(g, dy):
                return
            acc = accs[g]
            width = width_of(half)
            pairs = word_window(psum_s, g, dy, 0, half)[:].bitcast(BF16)
            for ep in range(2):
                for e in range(2):
                    k = (dy + PAD) * CS + ep - e + PAD
                    factor = alpha[:, 2 * g + e, k : k + 1]
                    if dy == -PAD and ep == 0:
                        nc.scalar.activation(
                            out=acc[e][:, half * HALF : (half + 1) * HALF],
                            in_=pixel_of_words(pairs, ep, HALF),
                            func=ACT.Copy,
                            scale=factor,
                        )
                    else:
                        prod = prod_pool.tile([P, HALF], F32, name="prod")
                        nc.scalar.activation(
                            out=prod[:, 0:width],
                            in_=pixel_of_words(pairs, ep, width),
                            func=ACT.Copy,
                            scale=factor,
                        )
                        nc.gpsimd.tensor_tensor(
                            out=acc[e][:, half * HALF : half * HALF + width],
                            in0=acc[e][:, half * HALF : half * HALF + width],
                            in1=prod[:, 0:width],
                            op=ALU.add,
                        )

        def vector_step(g, half, dy):
            acc = accs[g]
            width = width_of(half)
            terms = ([], [])
            for wsh in (-1, 0, 1):
                if wsh == 0 and middle_on_pool(g, dy):
                    continue
                pairs = word_window(psum_v, g, dy, wsh, half)[:].bitcast(BF16)
                for ep in range(2):
                    for e in range(2):
                        dx = 2 * wsh + ep - e
                        if abs(dx) <= PAD and (dx != 0 or dy != 0):
                            terms[e].append((pairs, ep, (dy + PAD) * CS + dx + PAD))
            for turn in zip(terms[0], terms[1]):
                for e in range(2):
                    pairs, ep, k = turn[e]
                    nc.vector.scalar_tensor_tensor(
                        out=acc[e][:, half * HALF : half * HALF + width],
                        in0=pixel_of_words(pairs, ep, width),
                        scalar=alpha[:, 2 * g + e, k : k + 1],
                        in1=acc[e][:, half * HALF : half * HALF + width],
                        op0=ALU.mult,
                        op1=ALU.add,
                    )

        def project(g):
            two = slice(2 * g, 2 * g + 2)
            dot = small.tile([P, 2], F32, name="dot")
            for e in range(2):
                scrap = scrap_pool.tile([P, C], F32, name="scrap")
                nc.vector.scalar_tensor_tensor(
                    out=scrap[:],
                    in0=pixel_of_words(f_own[:, g, :], e, C),
                    scalar=1.0,
                    in1=accs[g][e][:, 0:C],
                    op0=ALU.mult,
                    op1=ALU.mult,
                    accum_out=dot[:, e : e + 1],
                )
            gamma = small.tile([P, 2], F32, name="gamma")
            nc.vector.tensor_tensor(out=gamma[:], in0=dot[:], in1=rn2[:, two], op=ALU.mult)
            nc.vector.tensor_tensor(out=gamma[:], in0=centre[:, two], in1=gamma[:], op=ALU.subtract)
            gammas[g] = gamma

        def finish_step(g, half, j):
            b, d = divmod(g, GROUPS)
            lo = half * HALF
            if j < 2:
                e = j
                along = fin_pool.tile([P, HALF], F32, tag="along%d" % e, name="along%d" % e)
                nc.scalar.activation(
                    out=along[:],
                    in_=pixel_of_words(f_own[:, g, 2 * lo : 2 * (lo + HALF)], e, HALF),
                    func=ACT.Copy,
                    scale=gammas[g][:, e : e + 1],
                )
                bank = psum_mx.tile([P, HALF], F32, tag="dx", name="dx")
                dx_group(g, e, half, bank)
                dx_sb = fin_pool.tile([P, HALF], F32, tag="dx_sb%d" % e, name="dx_sb%d" % e)
                nc.scalar.copy(out=dx_sb[:], in_=bank[:])
                live[("parts", e)] = (accs[g][e][:, lo : lo + HALF], dx_sb[:], along[:])
            elif j < 4:
                if j == 2:
                    live["o_sb"] = fin_pool.tile([P, HALF // P, 2 * P], F32, tag="o_sb", name="o_sb")
                o_sb = live["o_sb"]
                first = 2 * (j - 2)
                o_ps = psum_o.tile([P, 2, 2, P], F32, tag="o", name="o_ps")
                for t2 in range(2):
                    t_cols = slice((first + t2) * P, (first + t2 + 1) * P)
                    for e in range(2):
                        parts = live[("parts", e)]
                        for i, part in enumerate(parts):
                            nc.tensor.matmul(
                                out=o_ps[:, t2, e, :],
                                lhsT=part[:, t_cols],
                                rhs=ident[:],
                                is_transpose=True,
                                start=(i == 0),
                                stop=(i == len(parts) - 1),
                            )
                nc.scalar.copy(
                    out=o_sb[:, first : first + 2, :].rearrange("p t (m e) -> p t m e", e=2),
                    in_=o_ps[:].rearrange("p t e m -> p t m e"),
                )
            else:
                o_sb = live["o_sb"]
                px = slice(2 * P * d, 2 * P * (d + 1))
                whole = HALF // P if half == 0 else HALF // P - 1
                nc.sync.dma_start(
                    out=res[b, lo : lo + whole * P, px].rearrange("(t p) x -> p t x", p=P),
                    in_=o_sb[:, 0:whole, :],
                )
                if half == 1:
                    nc.sync.dma_start(out=res[b, lo + whole * P : C, px], in_=o_sb[0:C_TAIL, whole, :])

        with tc.manual_schedule():
            for g in range(EARLY):
                load_gradient(g)
            for b in range(B):
                nc.sync.dma_start(out=scratch[b][0:MARGIN, :], in_=zeros[:])
                nc.sync.dma_start(out=scratch[b][MARGIN + HW : 2 * MARGIN + HW, :], in_=zeros[:])
            load_features(1)
            for s in range(STEPS):
                for g in range(EARLY):
                    prepare_step(g, s)
            load_gradient(EARLY)
            for i in range(-2, NG + 1):
                if EARLY < i + 5 < NG:
                    load_gradient(i + 5)
                for a in range(2):
                    for r in range(CS):
                        if EARLY <= i + 4 < NG:
                            prepare_step(i + 4, a * CS + r)
                        if 0 <= i + 2 < NG:
                            coeff_step(i + 2, a, r)
                        if 0 <= i + 1 < NG:
                            pool_step(i + 1, a, r - PAD)
                        if 0 <= i < NG:
                            vector_step(i, a, r - PAD)
                        if 0 <= i - 1 < NG:
                            finish_step(i - 1, a, r)
                if 0 <= i < NG:
                    project(i)
